import numpy as np
import ml_dtypes


def mxq(x, axis, fmt="e4m3"):
    dtype, down = {"e4m3": (ml_dtypes.float8_e4m3fn, 7), "e5m2": (ml_dtypes.float8_e5m2, 14)}[fmt]
    v = np.moveaxis(np.asarray(x, np.float32).astype(ml_dtypes.bfloat16).astype(np.float64), axis, -1)
    blocks = v.reshape(v.shape[:-1] + (-1, 32))
    amax = np.abs(blocks).max(-1, keepdims=True)
    byte = np.maximum(np.where(amax > 0, np.frexp(amax)[1] - 1 + 127, 0) - down, 1)
    scale = np.exp2(byte - 127.0)
    codes = (blocks / scale).astype(np.float32).astype(dtype).astype(np.float64)
    return np.moveaxis((codes * scale).reshape(v.shape), -1, axis)


WIDE = False


def mx_kscale(k):
    if not WIDE:
        return np.ones(k)
    levels = np.array([10, -10, 5, -5, 0])
    if k % 512:
        return np.exp2(np.random.permutation(np.resize(levels, k // 32))).repeat(32)
    a = np.empty((k // 512, 16))
    for p in range(k // 512):
        a[p, :8] = np.random.permutation(np.resize(levels, 8))
        for g in range(8):
            far = levels[np.abs(levels - a[p, g]) >= 10]
            a[p, g + 8] = far[np.random.randint(len(far))]
    return np.exp2(a.ravel()).repeat(32)


BF16 = ml_dtypes.bfloat16


def bf(x):
    return np.asarray(x, np.float32).astype(BF16)


def f64(x):
    return np.asarray(x).astype(np.float64)


B, T, H, KV, HD = 1, 512, 16, 4, 128
D = H * HD
KVD = KV * HD
O = D + 2 * KVD
ROPE_BASE = 500000.0
CLAMP = 8.0


def rope(u):
    n = u.shape[1]
    inv = 1.0 / ROPE_BASE ** (np.arange(0, HD, 2) / HD)
    freqs = np.arange(T)[:, None] * inv[None, :]
    cos, sin = np.cos(freqs)[None, None], np.sin(freqs)[None, None]
    p = u.reshape(B, n, T, HD // 2, 2)
    a, b = p[..., 0], p[..., 1]
    return np.stack([a * cos - b * sin, a * sin + b * cos], axis=-1).reshape(B, n, T, HD)


def draw0():
    s = mx_kscale(D)
    return {"x": bf(np.random.standard_normal((B, T, D)) * s),
            "w_qkv": bf(np.random.standard_normal((O, D)) * 0.5 * CLAMP / np.sqrt(D) / s[None, :])}


def core(x, w_qkv):
    qkv = mxq(f64(x), 2, "e4m3") @ mxq(f64(w_qkv), 1, "e4m3").T
    q = qkv[..., :D].reshape(B, T, H, HD).transpose(0, 2, 1, 3)
    k = qkv[..., D:D + KVD].reshape(B, T, KV, HD).transpose(0, 2, 1, 3)
    v = qkv[..., D + KVD:].reshape(B, T, KV, HD).transpose(0, 2, 1, 3)
    q = np.clip(rope(q), -CLAMP, CLAMP)
    k = np.clip(rope(k), -CLAMP, CLAMP)
    v = np.clip(v, -CLAMP, CLAMP)
    return q, k, v


def e4m3fn_bytes(y):
    return np.clip(np.asarray(y, np.float64), -448.0, 448.0).astype(np.float32).astype(ml_dtypes.float8_e4m3fn).view(np.uint8)


def e4m3fn_values(b):
    return np.asarray(b, np.uint8).view(ml_dtypes.float8_e4m3fn).astype(np.float64)


def setup_inputs():
    d = draw0()
    x0 = np.asarray(d['w_qkv']).astype(np.float64)
    s = (np.max(np.abs(x0), axis=(0,), keepdims=True) / 448.0).astype(np.float32)
    out = {}
    for k, v in d.items():
        if k == 'w_qkv':
            out['w_qkv_bytes'] = e4m3fn_bytes(x0 / s.astype(np.float64))
            out['w_qkv_scale'] = s
        else:
            out[k] = v
    return out


def reference(x, w_qkv_bytes, w_qkv_scale):
    return core(x, e4m3fn_values(w_qkv_bytes) * w_qkv_scale.astype(np.float64))

@@ -1,0 +1,319 @@
+from contextlib import ExitStack
+import math
+
+import concourse.mybir as mybir
+from concourse.masks import make_identity
+
+T, D, O = 512, 2048, 3072
+HD = 128
+FLOPS = 2 * T * D * O
+
+F32 = mybir.dt.float32
+BF16 = mybir.dt.bfloat16
+U32 = mybir.dt.uint32
+U8 = mybir.dt.uint8
+I32 = mybir.dt.int32
+FP8 = mybir.dt.float8_e4m3fn
+FP8X4 = mybir.dt.float8_e4m3fn_x4
+ALU = mybir.AluOpType
+ACT = mybir.ActivationFunctionType
+
+P = 128
+NG = 4
+NT = 4
+CLAMP = 8.0
+ROPE_BASE = 500000.0
+PI_HI = 3.140625
+PI_LO = math.pi - PI_HI
+
+
+def tile_dbrxattention_pa_kernel(tc, x, w_qkv_bytes, w_qkv_scale, out_0, out_1, out_2):
+    nc = tc.nc
+    with ExitStack() as ctx:
+        const = ctx.enter_context(tc.tile_pool(name="const", bufs=1))
+        wbp = ctx.enter_context(tc.tile_pool(name="wbp", bufs=4))
+        work = ctx.enter_context(tc.tile_pool(name="work", bufs=2))
+        psum = ctx.enter_context(tc.psum_pool(name="psum", bufs=4))
+        ctx.enter_context(tc.manual_schedule())
+
+        wb = {}
+        sc = const.tile([P, D], F32, name="sc", tag="sc")
+        s4 = const.tile([P, 4 * NG], F32, name="s4", tag="s4")
+        xs = work.tile([P, NT, D], BF16, name="xs", tag="big", bufs=2, align_bytes=64)
+
+        def load_w(cg, a0, a1):
+            if cg not in wb:
+                wb[cg] = wbp.tile([P, 4, D], U8, name="wbytes", tag="wbytes", bufs=4)
+            nc.sync.dma_start(
+                out=wb[cg][:, a0:a1, :],
+                in_=w_qkv_bytes[cg * 512 + a0 * P:cg * 512 + a1 * P, :].rearrange("(a p) k -> p a k", p=P),
+            )
+
+        tpos = const.tile([P, NT], F32, name="tpos", tag="tpos")
+        nc.gpsimd.iota(tpos[:], pattern=[[P, NT]], base=0, channel_multiplier=1,
+                       allow_small_or_imprecise_dtypes=True)
+        nc.gpsimd.dma_start(out=s4[:].rearrange("p (g t) -> p g t", t=4),
+                            in_=w_qkv_scale.rearrange("o (g p t) -> p (o g) t", p=P, t=4))
+        ident = const.tile([P, P], F32, name="ident", tag="ident")
+        make_identity(nc, ident[:])
+
+        def load_scales(lo, hi):
+            nc.sync.dma_start(out=sc[:, lo:hi],
+                              in_=w_qkv_scale[:, lo:hi].rearrange("o k -> (o k)").partition_broadcast(P))
+
+        load_w(0, 0, 1)
+        load_scales(0, D // 2)
+        load_w(4, 0, 1)
+        load_scales(D // 2, D)
+        for a in range(1, 4):
+            load_w(0, a, a + 1)
+            load_w(4, a, a + 1)
+        load_w(1, 0, 4)
+        for t in range(NT):
+            nc.sync.dma_start(out=xs[:, t, :], in_=x[0, t * P:(t + 1) * P, :])
+        load_w(2, 0, 4)
+        load_w(3, 0, 4)
+        load_w(5, 0, 4)
+
+        q = ROPE_BASE ** (-2.0 / HD)
+        angs = const.tile([P, 2, NT, 64], F32, name="angs", tag="angs")
+        nc.vector.tensor_copy(out=angs[:, 0, :, 0:1], in_=tpos[:].unsqueeze(2))
+        for j in range(6):
+            w = 2 ** j
+            nc.vector.tensor_scalar(out=angs[:, 0, :, w:2 * w], in0=angs[:, 0, :, 0:w], scalar1=q ** w,
+                                    scalar2=None, op0=ALU.mult)
+        nc.vector.tensor_scalar(out=angs[:, 1, :, :], in0=angs[:, 0, :, :], scalar1=0.5 * math.pi,
+                                scalar2=None, op0=ALU.add)
+        angf = angs[:].rearrange("p s t i -> p (s t i)")
+        turns = const.tile([P, 512], F32, name="turns", tag="turns")
+        nc.vector.tensor_scalar(out=turns[:], in0=angf, scalar1=1.0 / math.pi, scalar2=0.25,
+                                op0=ALU.mult, op1=ALU.add)
+        m_i = const.tile([P, 512], I32, name="m_i", tag="m_i")
+        nc.vector.tensor_copy(out=m_i[:], in_=turns[:])
+        red = const.tile([P, 512], F32, name="red", tag="red")
+        nc.vector.scalar_tensor_tensor(out=red[:], in0=m_i[:], scalar=-PI_HI, in1=angf,
+                                       op0=ALU.mult, op1=ALU.add)
+        red2 = const.tile([P, 512], F32, name="red2", tag="red2")
+        nc.vector.scalar_tensor_tensor(out=red2[:], in0=m_i[:], scalar=-PI_LO, in1=red[:],
+                                       op0=ALU.mult, op1=ALU.add)
+        sn = const.tile([P, 2, NT, 64], F32, name="sn", tag="sn")
+        nc.scalar.activation(out=sn[:].rearrange("p s t i -> p (s t i)"), in_=red2[:], func=ACT.Sin)
+        b_i = const.tile([P, 512], I32, name="b_i", tag="b_i")
+        nc.vector.tensor_scalar(out=b_i[:], in0=m_i[:], scalar1=1, scalar2=None, op0=ALU.bitwise_and)
+        sg = const.tile([P, 2, NT, 64], F32, name="sg", tag="sg")
+        nc.vector.tensor_scalar(out=sg[:].rearrange("p s t i -> p (s t i)"), in0=b_i[:], scalar1=-2.0,
+                                scalar2=1.0, op0=ALU.mult, op1=ALU.add)
+        tab = const.tile([P, NT, 2, 64, 2], F32, name="tab", tag="tab")
+
+        def tables_second_part():
+            for e in range(2):
+                nc.vector.tensor_tensor(out=tab[:, :, 0, :, e], in0=sn[:, 1, :, :], in1=sg[:, 1, :, :], op=ALU.mult)
+            nc.vector.tensor_tensor(out=tab[:, :, 1, :, 0], in0=sn[:, 0, :, :], in1=sg[:, 0, :, :], op=ALU.mult)
+            nc.vector.scalar_tensor_tensor(out=tab[:, :, 1, :, 1], in0=sn[:, 0, :, :], scalar=-1.0,
+                                           in1=sg[:, 0, :, :], op0=ALU.mult, op1=ALU.mult)
+
+        xc = const.tile([P, NG, T], U32, name="xc", tag="xc", align_bytes=64)
+        xsc = const.tile([P, NG, T], U8, name="xsc", tag="xsc", align_bytes=64)
+        wsc = {}
+        wbf = {}
+        grp = {}
+        wcod = {}
+        acc = {}
+
+        def scale_group(cg):
+            for a in range(4):
+                t = work.tile([P, D], BF16, name="wsc", tag="wsc", bufs=6)
+                pieces = 2 if (cg, a) == (0, 0) else 1
+                for c in range(pieces):
+                    cols = slice(c * D // pieces, (c + 1) * D // pieces)
+                    nc.vector.tensor_tensor(out=t[:, cols], in0=wb[cg][:, a, cols].bitcast(FP8), in1=sc[:, cols],
+                                            op=ALU.mult)
+                wsc[(cg, a)] = t
+
+        def new_groups(key):
+            if key == "x":
+                xg = work.tile([P, 2, 2, D], BF16, name="xg", tag="big", bufs=2, align_bytes=64)
+                grp[key] = [xg[:, h, :, :] for h in range(2)]
+            else:
+                grp[key] = [work.tile([P, 2, D], BF16, name="gr", tag="gr", bufs=4, align_bytes=64)[:]
+                            for h in range(2)]
+
+        def turn_pair(src0, src1, key, half):
+            words = [src0.bitcast(F32), src1.bitcast(F32)]
+            for g in range(NG):
+                bank = psum.tile([P, 512], F32, name="tr", tag="tr", bufs=4)
+                for a in range(2):
+                    for u in range(2):
+                        nc.tensor.transpose(bank[:, (2 * a + u) * P:(2 * a + u + 1) * P],
+                                            words[a][:, 256 * g + u:256 * (g + 1):2], ident[:])
+                nc.scalar.copy(
+                    out=grp[key][g // 2][:, g % 2, :].bitcast(F32)[:, half * 512:(half + 1) * 512].rearrange(
+                        "p (a r u) -> p a r u", a=2, u=2),
+                    in_=bank[:].rearrange("p (a u r) -> p a r u", a=2, u=2),
+                )
+
+        def turn_w(cg, half):
+            if half == 0:
+                new_groups(cg)
+            turn_pair(wsc[(cg, 2 * half)][:], wsc[(cg, 2 * half + 1)][:], cg, half)
+
+        def turn_x(half):
+            if half == 0:
+                new_groups("x")
+            turn_pair(xs[:, 2 * half, :], xs[:, 2 * half + 1, :], "x", half)
+
+        def cast_rows(cg, a):
+            t = work.tile([P, D], BF16, name="wbf", tag="wbf", bufs=4)
+            nc.scalar.copy(out=t[:], in_=wb[cg][:, a, :].bitcast(FP8))
+            wbf[(cg, a)] = t
+
+        def turn_scaled(cg, g):
+            if g == 0:
+                new_groups(cg)
+            planes = work.tile([P, 4, 512], BF16, name="planes", tag="planes", bufs=2)
+            for u in range(2):
+                bank = psum.tile([P, 512], F32, name="tr", tag="tr", bufs=4)
+                for a in range(4):
+                    nc.tensor.transpose(bank[:, a * P:(a + 1) * P],
+                                        wbf[(cg, a)][:].bitcast(F32)[:, 256 * g + u:256 * (g + 1):2], ident[:])
+                for e in range(2):
+                    j = 2 * u + e
+                    nc.scalar.activation(out=planes[:, j, :], in_=bank[:].bitcast(BF16)[:, e:1024:2],
+                                         func=ACT.Copy, scale=s4[:, 4 * g + j:4 * g + j + 1])
+            nc.scalar.copy(out=grp[cg][g // 2][:, g % 2, :].rearrange("p (r j) -> p r j", j=4),
+                           in_=planes[:].rearrange("p j r -> p r j"))
+
+        def quant_w(cg, halves=(0, 1)):
+            for h in halves:
+                c = work.tile([P, 2, 512], U32, name="wc", tag="wc", bufs=4, align_bytes=64)
+                s = work.tile([P, 2, 512], U8, name="ws", tag="ws", bufs=4, align_bytes=64)
+                nc.vector.quantize_mx(out=c[:].rearrange("p h c -> p (h c)").bitcast(FP8X4),
+                                      scales=s[:].rearrange("p h c -> p (h c)"),
+                                      in_=grp[cg][h].rearrange("p h c -> p (h c)"))
+                wcod[(cg, h)] = (c, s)
+
+        def quant_x():
+            for h in range(2):
+                nc.vector.quantize_mx(out=xc[:, 2 * h:2 * h + 2, :].rearrange("p h c -> p (h c)").bitcast(FP8X4),
+                                      scales=xsc[:, 2 * h:2 * h + 2, :].rearrange("p h c -> p (h c)"),
+                                      in_=grp["x"][h].rearrange("p h c -> p (h c)"))
+
+        def multiply(cg, tag, passes=(0, 1, 2, 3)):
+            for t in range(NT):
+                if passes[0] == 0:
+                    acc[(cg, t)] = psum.tile([P, 512], F32, name=tag, tag=tag, bufs=4)
+                for g in passes:
+                    c, s = wcod[(cg, g // 2)]
+                    nc.tensor.matmul_mx(
+                        out=acc[(cg, t)][:],
+                        lhsT=xc[:, g, t * P:(t + 1) * P].bitcast(FP8X4),
+                        lhsT_scale=xsc[:, g, t * P:(t + 1) * P],
+                        rhs=c[:, g % 2, :].bitcast(FP8X4),
+                        rhs_scale=s[:, g % 2, :],
+                        start=(g == 0),
+                        stop=(g == NG - 1),
+                    )
+
+        def store(cg, t, src):
+            if cg < 4:
+                dst = out_0[0, 4 * cg:4 * cg + 4, t * P:(t + 1) * P, :]
+            elif cg == 4:
+                dst = out_1[0, :, t * P:(t + 1) * P, :]
+            else:
+                dst = out_2[0, :, t * P:(t + 1) * P, :]
+            nc.sync.dma_start(out=dst.rearrange("n p h -> p n h"), in_=src.rearrange("p (n h) -> p n h", n=4))
+
+        prod = {}
+        res = {}
+
+        def rope_sum(engine, cg):
+            engine.tensor_tensor(
+                out=res[cg][:].rearrange("p t (m e) -> p t m e", e=2),
+                in0=prod[cg][:, :, 0, :].rearrange("p t (m e) -> p t m e", e=2),
+                in1=prod[cg][:, :, 1, :].rearrange("p t (m e) -> p t m e", e=2)[:, :, :, ::-1],
+                op=ALU.add)
+
+        def rope_products(cg, before):
+            prod[cg] = work.tile([P, NT, 2, 512], F32, name="prod", tag="big", bufs=2, align_bytes=64)
+            if before is not None:
+                res[before] = work.tile([P, NT, 512], F32, name="res", tag="res", bufs=3)
+                nc.vector.memset(res[before][:, 0, 0:1], 0.0)
+                rope_sum(nc.gpsimd, before)
+            for t in range(NT):
+                nc.vector.tensor_tensor(
+                    out=prod[cg][:, t, :, :].rearrange("p s (n h) -> p s n h", n=4),
+                    in0=acc[(cg, t)][:].rearrange("p (n h) -> p n h", n=4).unsqueeze(1).to_broadcast([P, 2, 4, HD]),
+                    in1=tab[:, t, :, :, :].rearrange("p s i e -> p s (i e)").unsqueeze(2).to_broadcast([P, 2, 4, HD]),
+                    op=ALU.mult)
+
+        def clamp_store(cg):
+            nc.vector.tensor_scalar(out=res[cg][:], in0=res[cg][:], scalar1=CLAMP, scalar2=-CLAMP,
+                                    op0=ALU.min, op1=ALU.max)
+            for t in range(NT):
+                store(cg, t, res[cg][:, t, :])
+
+        def finish_plain(cg):
+            for t in range(NT):
+                plain = work.tile([P, 512], F32, name="plain", tag="wbf", bufs=4)
+                nc.vector.tensor_scalar(out=plain[:], in0=acc[(cg, t)][:], scalar1=CLAMP, scalar2=-CLAMP,
+                                        op0=ALU.min, op1=ALU.max)
+                store(cg, t, plain[:])
+
+        scale_group(0)
+        cast_rows(4, 0)
+        cast_rows(4, 1)
+        turn_w(0, 0)
+        cast_rows(4, 2)
+        cast_rows(4, 3)
+        turn_w(0, 1)
+        tables_second_part()
+        scale_group(1)
+        turn_x(0)
+        turn_x(1)
+        quant_x()
+        turn_scaled(4, 0)
+        turn_w(1, 0)
+        turn_w(1, 1)
+        quant_w(0)
+        turn_scaled(4, 1)
+        multiply(0, "acc")
+        scale_group(2)
+        turn_scaled(4, 2)
+        turn_w(2, 0)
+        turn_w(2, 1)
+        quant_w(1)
+        rope_products(0, None)
+        turn_scaled(4, 3)
+        multiply(1, "acc")
+        scale_group(3)
+        cast_rows(5, 0)
+        turn_w(3, 0)
+        turn_w(3, 1)
+        for a in range(1, 4):
+            cast_rows(5, a)
+        quant_w(2)
+        rope_products(1, 0)
+        multiply(2, "acc")
+        turn_scaled(5, 0)
+        quant_w(4)
+        clamp_store(0)
+        turn_scaled(5, 1)
+        rope_products(2, 1)
+        multiply(4, "acc")
+        turn_scaled(5, 2)
+        quant_w(3)
+        clamp_store(1)
+        turn_scaled(5, 3)
+        rope_products(4, 2)
+        multiply(3, "acc")
+        clamp_store(2)
+        rope_products(3, 4)
+        quant_w(5, (0,))
+        multiply(5, "tr", (0, 1))
+        clamp_store(4)
+        res[3] = work.tile([P, NT, 512], F32, name="res", tag="res", bufs=3)
+        rope_sum(nc.vector, 3)
+        clamp_store(3)
+        quant_w(5, (1,))
+        multiply(5, "tr", (2, 3))
+        finish_plain(5)

@@ -75,6 +75,10 @@ def tile_dbrxattention_pa_kernel(tc, x, w_qkv_bytes, w_qkv_scale, out_0, out_1, 
         load_w(3, 0, 4)
         load_w(5, 0, 4)
 
+        warm = const.tile([P, 2], F32, name="warm", tag="warm")
+        nc.vector.memset(warm[:, 0:1], 0.0)
+        nc.scalar.activation(out=warm[:, 1:2], in_=warm[:, 0:1], func=ACT.Sin)
+
         q = ROPE_BASE ** (-2.0 / HD)
         angs = const.tile([P, 2, NT, 64], F32, name="angs", tag="angs")
         nc.vector.tensor_copy(out=angs[:, 0, :, 0:1], in_=tpos[:].unsqueeze(2))
@@ -85,32 +89,28 @@ def tile_dbrxattention_pa_kernel(tc, x, w_qkv_bytes, w_qkv_scale, out_0, out_1, 
         nc.vector.tensor_scalar(out=angs[:, 1, :, :], in0=angs[:, 0, :, :], scalar1=0.5 * math.pi,
                                 scalar2=None, op0=ALU.add)
         angf = angs[:].rearrange("p s t i -> p (s t i)")
-        turns = const.tile([P, 512], F32, name="turns", tag="turns")
-        nc.vector.tensor_scalar(out=turns[:], in0=angf, scalar1=1.0 / math.pi, scalar2=0.25,
-                                op0=ALU.mult, op1=ALU.add)
         m_i = const.tile([P, 512], I32, name="m_i", tag="m_i")
-        nc.vector.tensor_copy(out=m_i[:], in_=turns[:])
+        nc.vector.tensor_scalar(out=m_i[:], in0=angf, scalar1=1.0 / math.pi, scalar2=0.25,
+                                op0=ALU.mult, op1=ALU.add)
         red = const.tile([P, 512], F32, name="red", tag="red")
         nc.vector.scalar_tensor_tensor(out=red[:], in0=m_i[:], scalar=-PI_HI, in1=angf,
                                        op0=ALU.mult, op1=ALU.add)
         red2 = const.tile([P, 512], F32, name="red2", tag="red2")
         nc.vector.scalar_tensor_tensor(out=red2[:], in0=m_i[:], scalar=-PI_LO, in1=red[:],
                                        op0=ALU.mult, op1=ALU.add)
-        sn = const.tile([P, 2, NT, 64], F32, name="sn", tag="sn")
-        nc.scalar.activation(out=sn[:].rearrange("p s t i -> p (s t i)"), in_=red2[:], func=ACT.Sin)
         b_i = const.tile([P, 512], I32, name="b_i", tag="b_i")
         nc.vector.tensor_scalar(out=b_i[:], in0=m_i[:], scalar1=1, scalar2=None, op0=ALU.bitwise_and)
-        sg = const.tile([P, 2, NT, 64], F32, name="sg", tag="sg")
-        nc.vector.tensor_scalar(out=sg[:].rearrange("p s t i -> p (s t i)"), in0=b_i[:], scalar1=-2.0,
-                                scalar2=1.0, op0=ALU.mult, op1=ALU.add)
+        sg = const.tile([P, 512], F32, name="sg", tag="sg")
+        nc.vector.tensor_scalar(out=sg[:], in0=b_i[:], scalar1=-2.0, scalar2=1.0, op0=ALU.mult, op1=ALU.add)
+        arg = const.tile([P, 2, NT, 64], F32, name="arg", tag="arg")
+        nc.vector.tensor_tensor(out=arg[:].rearrange("p s t i -> p (s t i)"), in0=red2[:], in1=sg[:], op=ALU.mult)
         tab = const.tile([P, NT, 2, 64, 2], F32, name="tab", tag="tab")
 
         def tables_second_part():
             for e in range(2):
-                nc.vector.tensor_tensor(out=tab[:, :, 0, :, e], in0=sn[:, 1, :, :], in1=sg[:, 1, :, :], op=ALU.mult)
-            nc.vector.tensor_tensor(out=tab[:, :, 1, :, 0], in0=sn[:, 0, :, :], in1=sg[:, 0, :, :], op=ALU.mult)
-            nc.vector.scalar_tensor_tensor(out=tab[:, :, 1, :, 1], in0=sn[:, 0, :, :], scalar=-1.0,
-                                           in1=sg[:, 0, :, :], op0=ALU.mult, op1=ALU.mult)
+                nc.scalar.activation(out=tab[:, :, 0, :, e], in_=arg[:, 1, :, :], func=ACT.Sin)
+            nc.scalar.activation(out=tab[:, :, 1, :, 0], in_=arg[:, 0, :, :], func=ACT.Sin)
+            nc.scalar.activation(out=tab[:, :, 1, :, 1], in_=arg[:, 0, :, :], func=ACT.Sin, scale=-1.0)
 
         xc = const.tile([P, NG, T], U32, name="xc", tag="xc", align_bytes=64)
         xsc = const.tile([P, NG, T], U8, name="xsc", tag="xsc", align_bytes=64)
@@ -262,15 +262,15 @@ def tile_dbrxattention_pa_kernel(tc, x, w_qkv_bytes, w_qkv_scale, out_0, out_1, 
         scale_group(0)
         cast_rows(4, 0)
         cast_rows(4, 1)
+        tables_second_part()
         turn_w(0, 0)
         cast_rows(4, 2)
-        cast_rows(4, 3)
         turn_w(0, 1)
-        tables_second_part()
         scale_group(1)
         turn_x(0)
         turn_x(1)
         quant_x()
+        cast_rows(4, 3)
         turn_scaled(4, 0)
         turn_w(1, 0)
         turn_w(1, 1)

@@ -162,9 +162,12 @@ def tile_dbrxattention_pa_kernel(tc, x, w_qkv_bytes, w_qkv_scale, out_0, out_1, 
                 new_groups("x")
             turn_pair(xs[:, 2 * half, :], xs[:, 2 * half + 1, :], "x", half)
 
-        def cast_rows(cg, a):
+        def cast_rows(cg, a, on_vector=False):
             t = work.tile([P, D], BF16, name="wbf", tag="wbf", bufs=4)
-            nc.scalar.copy(out=t[:], in_=wb[cg][:, a, :].bitcast(FP8))
+            if on_vector:
+                nc.vector.tensor_copy(out=t[:], in_=wb[cg][:, a, :].bitcast(FP8))
+            else:
+                nc.scalar.copy(out=t[:], in_=wb[cg][:, a, :].bitcast(FP8))
             wbf[(cg, a)] = t
 
         def turn_scaled(cg, g):
@@ -289,9 +292,10 @@ def tile_dbrxattention_pa_kernel(tc, x, w_qkv_bytes, w_qkv_scale, out_0, out_1, 
         cast_rows(5, 0)
         turn_w(3, 0)
         turn_w(3, 1)
-        for a in range(1, 4):
-            cast_rows(5, a)
+        cast_rows(5, 1)
         quant_w(2)
+        cast_rows(5, 2, on_vector=True)
+        cast_rows(5, 3, on_vector=True)
         rope_products(1, 0)
         multiply(2, "acc")
         turn_scaled(5, 0)

@@ -293,8 +293,8 @@ def tile_dbrxattention_pa_kernel(tc, x, w_qkv_bytes, w_qkv_scale, out_0, out_1, 
         turn_w(3, 0)
         turn_w(3, 1)
         cast_rows(5, 1)
+        cast_rows(5, 2)
         quant_w(2)
-        cast_rows(5, 2, on_vector=True)
         cast_rows(5, 3, on_vector=True)
         rope_products(1, 0)
         multiply(2, "acc")

@@ -61,10 +61,9 @@ def tile_dbrxattention_pa_kernel(tc, x, w_qkv_bytes, w_qkv_scale, out_0, out_1, 
             nc.sync.dma_start(out=sc[:, lo:hi],
                               in_=w_qkv_scale[:, lo:hi].rearrange("o k -> (o k)").partition_broadcast(P))
 
-        load_w(0, 0, 1)
-        load_scales(0, D // 2)
         load_w(4, 0, 1)
-        load_scales(D // 2, D)
+        load_w(0, 0, 1)
+        load_scales(0, D)
         for a in range(1, 4):
             load_w(0, a, a + 1)
             load_w(4, a, a + 1)
@@ -123,7 +122,7 @@ def tile_dbrxattention_pa_kernel(tc, x, w_qkv_bytes, w_qkv_scale, out_0, out_1, 
         def scale_group(cg):
             for a in range(4):
                 t = work.tile([P, D], BF16, name="wsc", tag="wsc", bufs=6)
-                pieces = 2 if (cg, a) == (0, 0) else 1
+                pieces = 1
                 for c in range(pieces):
                     cols = slice(c * D // pieces, (c + 1) * D // pieces)
                     nc.vector.tensor_tensor(out=t[:, cols], in0=wb[cg][:, a, cols].bitcast(FP8), in1=sc[:, cols],

@@ -137,10 +137,20 @@ def tile_dbrxattention_pa_kernel(tc, x, w_qkv_bytes, w_qkv_scale, out_0, out_1, 
                 grp[key] = [work.tile([P, 2, D], BF16, name="gr", tag="gr", bufs=4, align_bytes=64)[:]
                             for h in range(2)]
 
+        ring = {"n": 0, "wide": True}
+
+        def tr_bank():
+            ring["n"] += 1
+            tag = "acc" if (ring["wide"] and ring["n"] % 2 == 0) else "tr"
+            return psum.tile([P, 512], F32, name=tag, tag=tag, bufs=4)
+
+        def narrow():
+            ring["wide"] = False
+
         def turn_pair(src0, src1, key, half):
             words = [src0.bitcast(F32), src1.bitcast(F32)]
             for g in range(NG):
-                bank = psum.tile([P, 512], F32, name="tr", tag="tr", bufs=4)
+                bank = tr_bank()
                 for a in range(2):
                     for u in range(2):
                         nc.tensor.transpose(bank[:, (2 * a + u) * P:(2 * a + u + 1) * P],
@@ -174,7 +184,7 @@ def tile_dbrxattention_pa_kernel(tc, x, w_qkv_bytes, w_qkv_scale, out_0, out_1, 
                 new_groups(cg)
             planes = work.tile([P, 4, 512], BF16, name="planes", tag="planes", bufs=2)
             for u in range(2):
-                bank = psum.tile([P, 512], F32, name="tr", tag="tr", bufs=4)
+                bank = tr_bank()
                 for a in range(4):
                     nc.tensor.transpose(bank[:, a * P:(a + 1) * P],
                                         wbf[(cg, a)][:].bitcast(F32)[:, 256 * g + u:256 * (g + 1):2], ident[:])
@@ -277,6 +287,7 @@ def tile_dbrxattention_pa_kernel(tc, x, w_qkv_bytes, w_qkv_scale, out_0, out_1, 
         turn_w(1, 0)
         turn_w(1, 1)
         quant_w(0)
+        narrow()
         turn_scaled(4, 1)
         multiply(0, "acc")
         scale_group(2)

@@ -52,8 +52,6 @@ def tile_dbrxattention_pa_kernel(tc, x, w_qkv_bytes, w_qkv_scale, out_0, out_1, 
         tpos = const.tile([P, NT], F32, name="tpos", tag="tpos")
         nc.gpsimd.iota(tpos[:], pattern=[[P, NT]], base=0, channel_multiplier=1,
                        allow_small_or_imprecise_dtypes=True)
-        nc.gpsimd.dma_start(out=s4[:].rearrange("p (g t) -> p g t", t=4),
-                            in_=w_qkv_scale.rearrange("o (g p t) -> p (o g) t", p=P, t=4))
         ident = const.tile([P, P], F32, name="ident", tag="ident")
         make_identity(nc, ident[:])
 
@@ -70,6 +68,8 @@ def tile_dbrxattention_pa_kernel(tc, x, w_qkv_bytes, w_qkv_scale, out_0, out_1, 
         load_w(1, 0, 4)
         for t in range(NT):
             nc.sync.dma_start(out=xs[:, t, :], in_=x[0, t * P:(t + 1) * P, :])
+        nc.sync.dma_start(out=s4[:].rearrange("p (g t) -> p g t", t=4),
+                          in_=w_qkv_scale.rearrange("o (g p t) -> p (o g) t", p=P, t=4))
         load_w(2, 0, 4)
         load_w(3, 0, 4)
         load_w(5, 0, 4)

@@ -27,27 +27,34 @@ PI_HI = 3.140625
 PI_LO = math.pi - PI_HI
 
 
+TAGS = {"trv": 3, "trs": 2, "acc": 3}
+WBF = 12
+
+
 def tile_dbrxattention_pa_kernel(tc, x, w_qkv_bytes, w_qkv_scale, out_0, out_1, out_2):
     nc = tc.nc
     with ExitStack() as ctx:
         const = ctx.enter_context(tc.tile_pool(name="const", bufs=1))
-        wbp = ctx.enter_context(tc.tile_pool(name="wbp", bufs=4))
         work = ctx.enter_context(tc.tile_pool(name="work", bufs=2))
         psum = ctx.enter_context(tc.psum_pool(name="psum", bufs=4))
         ctx.enter_context(tc.manual_schedule())
 
         wb = {}
-        sc = const.tile([P, D], F32, name="sc", tag="sc")
         s4 = const.tile([P, 4 * NG], F32, name="s4", tag="s4")
         xs = work.tile([P, NT, D], BF16, name="xs", tag="big", bufs=2, align_bytes=64)
+        nc.scalar.dma_start(out=s4[:].rearrange("p (g t) -> p g t", t=4),
+                            in_=w_qkv_scale.rearrange("o (g p t) -> p (o g) t", p=P, t=4))
 
         def load_w(cg, a0, a1):
             if cg not in wb:
-                wb[cg] = wbp.tile([P, 4, D], U8, name="wbytes", tag="wbytes", bufs=4)
+                wb[cg] = work.tile([P, 4, D], U8, name="wbytes", tag="wbytes", bufs=4)
             nc.sync.dma_start(
                 out=wb[cg][:, a0:a1, :],
                 in_=w_qkv_bytes[cg * 512 + a0 * P:cg * 512 + a1 * P, :].rearrange("(a p) k -> p a k", p=P),
             )
+
+        def load_x(t):
+            nc.sync.dma_start(out=xs[:, t, :], in_=x[0, t * P:(t + 1) * P, :])
 
         tpos = const.tile([P, NT], F32, name="tpos", tag="tpos")
         nc.gpsimd.iota(tpos[:], pattern=[[P, NT]], base=0, channel_multiplier=1,
@@ -55,23 +62,18 @@ def tile_dbrxattention_pa_kernel(tc, x, w_qkv_bytes, w_qkv_scale, out_0, out_1, 
         ident = const.tile([P, P], F32, name="ident", tag="ident")
         make_identity(nc, ident[:])
 
-        def load_scales(lo, hi):
-            nc.sync.dma_start(out=sc[:, lo:hi],
-                              in_=w_qkv_scale[:, lo:hi].rearrange("o k -> (o k)").partition_broadcast(P))
-
-        load_w(4, 0, 1)
         load_w(0, 0, 1)
-        load_scales(0, D)
-        for a in range(1, 4):
-            load_w(0, a, a + 1)
-            load_w(4, a, a + 1)
+        load_w(0, 1, 2)
+        load_w(0, 2, 3)
+        load_w(0, 3, 4)
+        load_x(0)
+        load_x(1)
+        load_x(2)
+        load_x(3)
         load_w(1, 0, 4)
-        for t in range(NT):
-            nc.sync.dma_start(out=xs[:, t, :], in_=x[0, t * P:(t + 1) * P, :])
-        nc.sync.dma_start(out=s4[:].rearrange("p (g t) -> p g t", t=4),
-                          in_=w_qkv_scale.rearrange("o (g p t) -> p (o g) t", p=P, t=4))
         load_w(2, 0, 4)
         load_w(3, 0, 4)
+        load_w(4, 0, 4)
         load_w(5, 0, 4)
 
         warm = const.tile([P, 2], F32, name="warm", tag="warm")
@@ -106,125 +108,121 @@ def tile_dbrxattention_pa_kernel(tc, x, w_qkv_bytes, w_qkv_scale, out_0, out_1, 
         tab = const.tile([P, NT, 2, 64, 2], F32, name="tab", tag="tab")
 
         def tables_second_part():
-            for e in range(2):
-                nc.scalar.activation(out=tab[:, :, 0, :, e], in_=arg[:, 1, :, :], func=ACT.Sin)
+            nc.scalar.activation(
+                out=tab[:, :, 0, :, :].rearrange("p t i e -> p t (i e)").rearrange("p t (i e) -> p t i e", e=2),
+                in_=arg[:, 1, :, :].unsqueeze(3).to_broadcast([P, NT, 64, 2]), func=ACT.Sin)
             nc.scalar.activation(out=tab[:, :, 1, :, 0], in_=arg[:, 0, :, :], func=ACT.Sin)
             nc.scalar.activation(out=tab[:, :, 1, :, 1], in_=arg[:, 0, :, :], func=ACT.Sin, scale=-1.0)
 
         xc = const.tile([P, NG, T], U32, name="xc", tag="xc", align_bytes=64)
         xsc = const.tile([P, NG, T], U8, name="xsc", tag="xsc", align_bytes=64)
-        wsc = {}
         wbf = {}
         grp = {}
         wcod = {}
         acc = {}
+        planes = {}
+        xgrp = []
 
-        def scale_group(cg):
-            for a in range(4):
-                t = work.tile([P, D], BF16, name="wsc", tag="wsc", bufs=6)
-                pieces = 1
-                for c in range(pieces):
-                    cols = slice(c * D // pieces, (c + 1) * D // pieces)
-                    nc.vector.tensor_tensor(out=t[:, cols], in0=wb[cg][:, a, cols].bitcast(FP8), in1=sc[:, cols],
-                                            op=ALU.mult)
-                wsc[(cg, a)] = t
-
-        def new_groups(key):
-            if key == "x":
-                xg = work.tile([P, 2, 2, D], BF16, name="xg", tag="big", bufs=2, align_bytes=64)
-                grp[key] = [xg[:, h, :, :] for h in range(2)]
+        def cast(cg, a, engine, held=False):
+            t = work.tile([P, D], BF16, name="wbf", tag="wbf", bufs=WBF)
+            if held:
+                nc.vector.memset(t[:, 0:2], 0.0)
+            src = wb[cg][:, a, :].bitcast(FP8)
+            if engine is nc.scalar:
+                nc.scalar.copy(out=t[:], in_=src)
             else:
-                grp[key] = [work.tile([P, 2, D], BF16, name="gr", tag="gr", bufs=4, align_bytes=64)[:]
-                            for h in range(2)]
-
-        ring = {"n": 0, "wide": True}
-
-        def tr_bank():
-            ring["n"] += 1
-            tag = "acc" if (ring["wide"] and ring["n"] % 2 == 0) else "tr"
-            return psum.tile([P, 512], F32, name=tag, tag=tag, bufs=4)
-
-        def narrow():
-            ring["wide"] = False
-
-        def turn_pair(src0, src1, key, half):
-            words = [src0.bitcast(F32), src1.bitcast(F32)]
-            for g in range(NG):
-                bank = tr_bank()
-                for a in range(2):
-                    for u in range(2):
-                        nc.tensor.transpose(bank[:, (2 * a + u) * P:(2 * a + u + 1) * P],
-                                            words[a][:, 256 * g + u:256 * (g + 1):2], ident[:])
-                nc.scalar.copy(
-                    out=grp[key][g // 2][:, g % 2, :].bitcast(F32)[:, half * 512:(half + 1) * 512].rearrange(
-                        "p (a r u) -> p a r u", a=2, u=2),
-                    in_=bank[:].rearrange("p (a u r) -> p a r u", a=2, u=2),
-                )
-
-        def turn_w(cg, half):
-            if half == 0:
-                new_groups(cg)
-            turn_pair(wsc[(cg, 2 * half)][:], wsc[(cg, 2 * half + 1)][:], cg, half)
-
-        def turn_x(half):
-            if half == 0:
-                new_groups("x")
-            turn_pair(xs[:, 2 * half, :], xs[:, 2 * half + 1, :], "x", half)
-
-        def cast_rows(cg, a, on_vector=False):
-            t = work.tile([P, D], BF16, name="wbf", tag="wbf", bufs=4)
-            if on_vector:
-                nc.vector.tensor_copy(out=t[:], in_=wb[cg][:, a, :].bitcast(FP8))
-            else:
-                nc.scalar.copy(out=t[:], in_=wb[cg][:, a, :].bitcast(FP8))
+                engine.tensor_copy(out=t[:], in_=src)
             wbf[(cg, a)] = t
 
-        def turn_scaled(cg, g):
-            if g == 0:
-                new_groups(cg)
-            planes = work.tile([P, 4, 512], BF16, name="planes", tag="planes", bufs=2)
-            for u in range(2):
-                bank = tr_bank()
-                for a in range(4):
-                    nc.tensor.transpose(bank[:, a * P:(a + 1) * P],
-                                        wbf[(cg, a)][:].bitcast(F32)[:, 256 * g + u:256 * (g + 1):2], ident[:])
-                for e in range(2):
-                    j = 2 * u + e
-                    nc.scalar.activation(out=planes[:, j, :], in_=bank[:].bitcast(BF16)[:, e:1024:2],
-                                         func=ACT.Copy, scale=s4[:, 4 * g + j:4 * g + j + 1])
-            nc.scalar.copy(out=grp[cg][g // 2][:, g % 2, :].rearrange("p (r j) -> p r j", j=4),
-                           in_=planes[:].rearrange("p j r -> p r j"))
+        def half_tile(cg, h):
+            if (cg, h) not in grp:
+                grp[(cg, h)] = work.tile([P, 2, D], BF16, name="gr", tag="gr%d" % h, bufs=2, align_bytes=64)
+            return grp[(cg, h)]
 
-        def quant_w(cg, halves=(0, 1)):
-            for h in halves:
-                c = work.tile([P, 2, 512], U32, name="wc", tag="wc", bufs=4, align_bytes=64)
-                s = work.tile([P, 2, 512], U8, name="ws", tag="ws", bufs=4, align_bytes=64)
-                nc.vector.quantize_mx(out=c[:].rearrange("p h c -> p (h c)").bitcast(FP8X4),
-                                      scales=s[:].rearrange("p h c -> p (h c)"),
-                                      in_=grp[cg][h].rearrange("p h c -> p (h c)"))
-                wcod[(cg, h)] = (c, s)
+        vb = {}
+        sb = {}
+
+        def vtr(cg, g, h, tag="trv"):
+            bank = psum.tile([P, 512], F32, name=tag, tag=tag, bufs=TAGS[tag])
+            vb[(cg, g, h)] = bank
+            for u in range(2):
+                for a in range(2):
+                    nc.tensor.transpose(bank[:, (2 * u + a) * P:(2 * u + a + 1) * P],
+                                        wbf[(cg, 2 * h + a)][:].bitcast(F32)[:, 256 * g + u:256 * (g + 1):2], ident[:])
+
+        def vop(cg, g, h):
+            gr = half_tile(cg, g // 2)
+            bank = vb[(cg, g, h)]
+            nc.vector.tensor_tensor(
+                out=gr[:, g % 2, h * 1024:(h + 1) * 1024].rearrange("p (r u e) -> p r u e", u=2, e=2),
+                in0=bank[:].bitcast(BF16).rearrange("p (u r e) -> p r u e", u=2, e=2),
+                in1=s4[:, 4 * g:4 * g + 4].rearrange("p (u e) -> p u e", e=2).unsqueeze(1).to_broadcast([P, 256, 2, 2]),
+                op=ALU.mult)
+
+        def st(cg, g, u, tag="trs"):
+            bank = psum.tile([P, 512], F32, name=tag, tag=tag, bufs=TAGS[tag])
+            sb[(cg, g, u)] = bank
+            for a in range(4):
+                nc.tensor.transpose(bank[:, a * P:(a + 1) * P],
+                                    wbf[(cg, a)][:].bitcast(F32)[:, 256 * g + u:256 * (g + 1):2], ident[:])
+
+        def sop(cg, g, u):
+            gr = half_tile(cg, g // 2)
+            if u == 0:
+                planes[(cg, g)] = work.tile([P, 4, 512], BF16, name="planes", tag="planes", bufs=2)
+            pl = planes[(cg, g)]
+            bank = sb[(cg, g, u)]
+            for e in range(2):
+                j = 2 * u + e
+                nc.scalar.activation(out=pl[:, j, :], in_=bank[:].bitcast(BF16)[:, e:1024:2],
+                                     func=ACT.Copy, scale=s4[:, 4 * g + j:4 * g + j + 1])
+            if u == 1:
+                nc.scalar.copy(out=gr[:, g % 2, :].rearrange("p (c i j) -> p c j i", i=4, j=4),
+                               in_=pl[:].rearrange("p j (c i) -> p c j i", i=4))
+
+        def xbank(half, g):
+            if not xgrp:
+                xgrp.append(work.tile([P, 2, 2, D], BF16, name="xg", tag="big", bufs=2, align_bytes=64))
+            tag = "trs"
+            bank = psum.tile([P, 512], F32, name=tag, tag=tag, bufs=TAGS[tag])
+            for a in range(2):
+                for u in range(2):
+                    nc.tensor.transpose(bank[:, (2 * a + u) * P:(2 * a + u + 1) * P],
+                                        xs[:, 2 * half + a, :].bitcast(F32)[:, 256 * g + u:256 * (g + 1):2], ident[:])
+            nc.scalar.copy(
+                out=xgrp[0][:, g // 2, g % 2, :].bitcast(F32)[:, half * 512:(half + 1) * 512].rearrange(
+                    "p (a r u) -> p a r u", a=2, u=2),
+                in_=bank[:].rearrange("p (a u r) -> p a r u", a=2, u=2),
+            )
 
         def quant_x():
             for h in range(2):
                 nc.vector.quantize_mx(out=xc[:, 2 * h:2 * h + 2, :].rearrange("p h c -> p (h c)").bitcast(FP8X4),
                                       scales=xsc[:, 2 * h:2 * h + 2, :].rearrange("p h c -> p (h c)"),
-                                      in_=grp["x"][h].rearrange("p h c -> p (h c)"))
+                                      in_=xgrp[0][:, h, :, :].rearrange("p h c -> p (h c)"))
 
-        def multiply(cg, tag, passes=(0, 1, 2, 3)):
-            for t in range(NT):
-                if passes[0] == 0:
-                    acc[(cg, t)] = psum.tile([P, 512], F32, name=tag, tag=tag, bufs=4)
-                for g in passes:
-                    c, s = wcod[(cg, g // 2)]
-                    nc.tensor.matmul_mx(
-                        out=acc[(cg, t)][:],
-                        lhsT=xc[:, g, t * P:(t + 1) * P].bitcast(FP8X4),
-                        lhsT_scale=xsc[:, g, t * P:(t + 1) * P],
-                        rhs=c[:, g % 2, :].bitcast(FP8X4),
-                        rhs_scale=s[:, g % 2, :],
-                        start=(g == 0),
-                        stop=(g == NG - 1),
-                    )
+        def quant_w(cg, h):
+            c = work.tile([P, 2, 512], U32, name="wc", tag="wc", bufs=4, align_bytes=64)
+            s = work.tile([P, 2, 512], U8, name="ws", tag="ws", bufs=4, align_bytes=64)
+            nc.vector.quantize_mx(out=c[:].rearrange("p h c -> p (h c)").bitcast(FP8X4),
+                                  scales=s[:].rearrange("p h c -> p (h c)"),
+                                  in_=grp[(cg, h)][:].rearrange("p h c -> p (h c)"))
+            wcod[(cg, h)] = (c, s)
+
+        def multiply(cg, t, passes=(0, 1, 2, 3), tag="acc"):
+            if passes[0] == 0:
+                acc[(cg, t)] = psum.tile([P, 512], F32, name=tag, tag=tag, bufs=TAGS[tag])
+            for g in passes:
+                c, s = wcod[(cg, g // 2)]
+                nc.tensor.matmul_mx(
+                    out=acc[(cg, t)][:],
+                    lhsT=xc[:, g, t * P:(t + 1) * P].bitcast(FP8X4),
+                    lhsT_scale=xsc[:, g, t * P:(t + 1) * P],
+                    rhs=c[:, g % 2, :].bitcast(FP8X4),
+                    rhs_scale=s[:, g % 2, :],
+                    start=(g == 0),
+                    stop=(g == NG - 1),
+                )
 
         def store(cg, t, src):
             if cg < 4:
@@ -238,96 +236,131 @@ def tile_dbrxattention_pa_kernel(tc, x, w_qkv_bytes, w_qkv_scale, out_0, out_1, 
         prod = {}
         res = {}
 
-        def rope_sum(engine, cg):
+        def rope_product(cg, t):
+            if t == 0:
+                prod[cg] = work.tile([P, NT, 2, 512], F32, name="prod", tag="big", bufs=2, align_bytes=64)
+            nc.vector.tensor_tensor(
+                out=prod[cg][:, t, :, :].rearrange("p s (n h) -> p s n h", n=4),
+                in0=acc[(cg, t)][:].rearrange("p (n h) -> p n h", n=4).unsqueeze(1).to_broadcast([P, 2, 4, HD]),
+                in1=tab[:, t, :, :, :].rearrange("p s i e -> p s (i e)").unsqueeze(2).to_broadcast([P, 2, 4, HD]),
+                op=ALU.mult)
+
+        def rope_sum(engine, cg, t0, t1):
             engine.tensor_tensor(
-                out=res[cg][:].rearrange("p t (m e) -> p t m e", e=2),
-                in0=prod[cg][:, :, 0, :].rearrange("p t (m e) -> p t m e", e=2),
-                in1=prod[cg][:, :, 1, :].rearrange("p t (m e) -> p t m e", e=2)[:, :, :, ::-1],
+                out=res[cg][:, t0:t1, :].rearrange("p t (m e) -> p t m e", e=2),
+                in0=prod[cg][:, t0:t1, 0, :].rearrange("p t (m e) -> p t m e", e=2),
+                in1=prod[cg][:, t0:t1, 1, :].rearrange("p t (m e) -> p t m e", e=2)[:, :, :, ::-1],
                 op=ALU.add)
 
-        def rope_products(cg, before):
-            prod[cg] = work.tile([P, NT, 2, 512], F32, name="prod", tag="big", bufs=2, align_bytes=64)
-            if before is not None:
-                res[before] = work.tile([P, NT, 512], F32, name="res", tag="res", bufs=3)
-                nc.vector.memset(res[before][:, 0, 0:1], 0.0)
-                rope_sum(nc.gpsimd, before)
-            for t in range(NT):
-                nc.vector.tensor_tensor(
-                    out=prod[cg][:, t, :, :].rearrange("p s (n h) -> p s n h", n=4),
-                    in0=acc[(cg, t)][:].rearrange("p (n h) -> p n h", n=4).unsqueeze(1).to_broadcast([P, 2, 4, HD]),
-                    in1=tab[:, t, :, :, :].rearrange("p s i e -> p s (i e)").unsqueeze(2).to_broadcast([P, 2, 4, HD]),
-                    op=ALU.mult)
-
-        def clamp_store(cg):
-            nc.vector.tensor_scalar(out=res[cg][:], in0=res[cg][:], scalar1=CLAMP, scalar2=-CLAMP,
-                                    op0=ALU.min, op1=ALU.max)
-            for t in range(NT):
+        def clamp_store(engine, cg, t0, t1):
+            engine.tensor_scalar(out=res[cg][:, t0:t1, :], in0=res[cg][:, t0:t1, :], scalar1=CLAMP, scalar2=-CLAMP,
+                                 op0=ALU.min, op1=ALU.max)
+            for t in range(t0, t1):
                 store(cg, t, res[cg][:, t, :])
 
-        def finish_plain(cg):
-            for t in range(NT):
-                plain = work.tile([P, 512], F32, name="plain", tag="wbf", bufs=4)
-                nc.vector.tensor_scalar(out=plain[:], in0=acc[(cg, t)][:], scalar1=CLAMP, scalar2=-CLAMP,
-                                        op0=ALU.min, op1=ALU.max)
-                store(cg, t, plain[:])
+        def new_res(cg):
+            res[cg] = work.tile([P, NT, 512], F32, name="res", tag="res", bufs=3)
 
-        scale_group(0)
-        cast_rows(4, 0)
-        cast_rows(4, 1)
+        def release(cg):
+            new_res(cg)
+            nc.vector.memset(res[cg][:, 0, 0:1], 0.0)
+
+        def finish_plain(cg, t):
+            plain = work.tile([P, 512], F32, name="plain", tag="plain", bufs=4)
+            nc.vector.tensor_scalar(out=plain[:], in0=acc[(cg, t)][:], scalar1=CLAMP, scalar2=-CLAMP,
+                                    op0=ALU.min, op1=ALU.max)
+            store(cg, t, plain[:])
+
+        V, S, G = nc.vector, nc.scalar, nc.gpsimd
+        NV = [4,2,2,2,2,2]
+
+        def vbanks(cg):
+            return [(g, h) for g in range(NV[cg]) for h in range(2)]
+
+        def sbanks(cg):
+            return [(g, u) for g in range(NV[cg], 4) for u in range(2)]
+
+        for a in range(4):
+            cast(0, a, S)
+        for g in range(NG):
+            vtr(0, g, 0, "trv" if g % 2 == 0 else "acc")
+        for g in range(NG):
+            vop(0, g, 0)
+        for g in range(NG):
+            xbank(0, g)
+        for g in range(NG):
+            vtr(0, g, 1, "trv" if g % 2 == 0 else "acc")
+        for g in range(NG):
+            vop(0, g, 1)
         tables_second_part()
-        turn_w(0, 0)
-        cast_rows(4, 2)
-        turn_w(0, 1)
-        scale_group(1)
-        turn_x(0)
-        turn_x(1)
+        for g in range(NG):
+            xbank(1, g)
+        cast(1, 2, G)
+        cast(1, 0, S)
+        cast(1, 1, S)
+        cast(1, 3, G)
+        cast(2, 0, S)
         quant_x()
-        cast_rows(4, 3)
-        turn_scaled(4, 0)
-        turn_w(1, 0)
-        turn_w(1, 1)
-        quant_w(0)
-        narrow()
-        turn_scaled(4, 1)
-        multiply(0, "acc")
-        scale_group(2)
-        turn_scaled(4, 2)
-        turn_w(2, 0)
-        turn_w(2, 1)
-        quant_w(1)
-        rope_products(0, None)
-        turn_scaled(4, 3)
-        multiply(1, "acc")
-        scale_group(3)
-        cast_rows(5, 0)
-        turn_w(3, 0)
-        turn_w(3, 1)
-        cast_rows(5, 1)
-        cast_rows(5, 2)
-        quant_w(2)
-        cast_rows(5, 3, on_vector=True)
-        rope_products(1, 0)
-        multiply(2, "acc")
-        turn_scaled(5, 0)
-        quant_w(4)
-        clamp_store(0)
-        turn_scaled(5, 1)
-        rope_products(2, 1)
-        multiply(4, "acc")
-        turn_scaled(5, 2)
-        quant_w(3)
-        clamp_store(1)
-        turn_scaled(5, 3)
-        rope_products(4, 2)
-        multiply(3, "acc")
-        clamp_store(2)
-        rope_products(3, 4)
-        quant_w(5, (0,))
-        multiply(5, "tr", (0, 1))
-        clamp_store(4)
-        res[3] = work.tile([P, NT, 512], F32, name="res", tag="res", bufs=3)
-        rope_sum(nc.vector, 3)
-        clamp_store(3)
-        quant_w(5, (1,))
-        multiply(5, "tr", (2, 3))
-        finish_plain(5)
+        quant_w(0, 0)
+        for b in sbanks(1)[:2]:
+            st(1, *b)
+        for b in vbanks(1)[:3]:
+            vtr(1, *b)
+        for cg in range(5):
+            nx = cg + 1
+            fu = cg + 2
+            vb_ = vbanks(nx)
+            sb_ = sbanks(nx)
+            if cg > 0:
+                quant_w(cg, 0)
+            quant_w(cg, 1)
+            if cg >= 1:
+                release(cg - 1)
+                rope_sum(G, cg - 1, 0, 4)
+                clamp_store(G, cg - 1, 0, 4)
+                if cg + 3 < 6:
+                    cast(cg + 3, 3, G)
+            else:
+                cast(2, 2, G, True)
+                cast(2, 3, G)
+                cast(3, 3, G)
+            casts = [(cg + 3, a) for a in range(3)] if cg + 3 < 6 else []
+            if cg == 0:
+                casts = [(2, 1)] + casts
+            for i in range(8):
+                if i < len(vb_):
+                    vop(nx, *vb_[i])
+                if i + 3 < len(vb_):
+                    vtr(nx, *vb_[i + 3])
+                if i < len(sb_):
+                    sop(nx, *sb_[i])
+                if i < 3:
+                    multiply(cg, i)
+                if i + 2 < len(sb_):
+                    st(nx, *sb_[i + 2])
+                if i == 1:
+                    for c in casts:
+                        cast(*c, S)
+            rope_product(cg, 0)
+            multiply(cg, 3)
+            if fu < 6:
+                for b in vbanks(fu)[:3]:
+                    vtr(fu, *b)
+                for b in sbanks(fu)[:2]:
+                    st(fu, *b)
+            for t in range(1, NT):
+                rope_product(cg, t)
+        new_res(4)
+        rope_sum(V, 4, 0, 3)
+        quant_w(5, 0)
+        tags = ["trv", "trv", "trv", "trs"]
+        for t in range(NT):
+            multiply(5, t, (0, 1), tags[t])
+        quant_w(5, 1)
+        clamp_store(V, 4, 0, 3)
+        nc.vector.memset(res[4][:, 3, 0:1], 0.0)
+        rope_sum(G, 4, 3, 4)
+        clamp_store(G, 4, 3, 4)
+        for t in range(NT):
+            multiply(5, t, (2, 3))
+            finish_plain(5, t)

@@ -28,7 +28,7 @@ PI_LO = math.pi - PI_HI
 
 
 TAGS = {"trv": 3, "trs": 2, "acc": 3}
-WBF = 12
+WBF = 11
 
 
 def tile_dbrxattention_pa_kernel(tc, x, w_qkv_bytes, w_qkv_scale, out_0, out_1, out_2):
@@ -42,8 +42,8 @@ def tile_dbrxattention_pa_kernel(tc, x, w_qkv_bytes, w_qkv_scale, out_0, out_1, 
         wb = {}
         s4 = const.tile([P, 4 * NG], F32, name="s4", tag="s4")
         xs = work.tile([P, NT, D], BF16, name="xs", tag="big", bufs=2, align_bytes=64)
-        nc.scalar.dma_start(out=s4[:].rearrange("p (g t) -> p g t", t=4),
-                            in_=w_qkv_scale.rearrange("o (g p t) -> p (o g) t", p=P, t=4))
+        nc.sync.dma_start(out=s4[:].rearrange("p (g t) -> p g t", t=4),
+                          in_=w_qkv_scale.rearrange("o (g p t) -> p (o g) t", p=P, t=4))
 
         def load_w(cg, a0, a1):
             if cg not in wb:
@@ -166,19 +166,36 @@ def tile_dbrxattention_pa_kernel(tc, x, w_qkv_bytes, w_qkv_scale, out_0, out_1, 
                 nc.tensor.transpose(bank[:, a * P:(a + 1) * P],
                                     wbf[(cg, a)][:].bitcast(F32)[:, 256 * g + u:256 * (g + 1):2], ident[:])
 
-        def sop(cg, g, u):
-            gr = half_tile(cg, g // 2)
+        identb = const.tile([P, P], BF16, name="identb", tag="identb")
+        make_identity(nc, identb[:])
+        ib = {}
+
+        def acts(cg, g, u):
             if u == 0:
-                planes[(cg, g)] = work.tile([P, 4, 512], BF16, name="planes", tag="planes", bufs=2)
+                planes[(cg, g)] = work.tile([P, 4, 512], BF16, name="planes", tag="planes", bufs=3)
             pl = planes[(cg, g)]
             bank = sb[(cg, g, u)]
             for e in range(2):
                 j = 2 * u + e
                 nc.scalar.activation(out=pl[:, j, :], in_=bank[:].bitcast(BF16)[:, e:1024:2],
                                      func=ACT.Copy, scale=s4[:, 4 * g + j:4 * g + j + 1])
-            if u == 1:
-                nc.scalar.copy(out=gr[:, g % 2, :].rearrange("p (c i j) -> p c j i", i=4, j=4),
-                               in_=pl[:].rearrange("p j (c i) -> p c j i", i=4))
+
+        def weave_scalar(cg, g):
+            gr = half_tile(cg, g // 2)
+            nc.scalar.copy(out=gr[:, g % 2, :].rearrange("p (r j) -> p r j", j=4),
+                           in_=planes[(cg, g)][:].rearrange("p j r -> p r j"))
+
+        def weave_tensor(cg, g, c):
+            bank = psum.tile([P, 1024], BF16, name="trs", tag="trs", bufs=TAGS["trs"])
+            ib[(cg, g, c)] = bank
+            for q in range(2):
+                rows = slice((2 * c + q) * P, (2 * c + q + 1) * P)
+                nc.tensor.matmul(bank[:, q * 512:(q + 1) * 512].rearrange("p (r j) -> p r j", j=4), lhsT=identb[:],
+                                 rhs=planes[(cg, g)][:, :, rows].rearrange("p j r -> p r j"), start=True, stop=True)
+
+        def weave_out(cg, g, c):
+            gr = half_tile(cg, g // 2)
+            nc.scalar.copy(out=gr[:, g % 2, c * 1024:(c + 1) * 1024], in_=ib[(cg, g, c)][:])
 
         def xbank(half, g):
             if not xgrp:
@@ -272,13 +289,16 @@ def tile_dbrxattention_pa_kernel(tc, x, w_qkv_bytes, w_qkv_scale, out_0, out_1, 
             store(cg, t, plain[:])
 
         V, S, G = nc.vector, nc.scalar, nc.gpsimd
-        NV = [4,2,2,2,2,2]
+        NV = [4,2,3,2,2,1]
+        SL = [2,2,2,2,2]
+        CAST = [{"G":[[2,2],[2,3],[3,3]],"S":[[2,1],[3,0],[3,1],[3,2]]},{"G":[[4,3]],"S":[[4,0],[4,1],[4,2]]},{"G":[[5,3]],"S":[[5,0],[5,1],[5,2]]},{"G":[],"S":[]},{"G":[],"S":[]}]
+        PI = lambda cg, g: False
 
         def vbanks(cg):
             return [(g, h) for g in range(NV[cg]) for h in range(2)]
 
-        def sbanks(cg):
-            return [(g, u) for g in range(NV[cg], 4) for u in range(2)]
+        stream = [(cg, g) for cg in range(1, 6) for g in range(NV[cg], 4)]
+        bounds = [sum(SL[:i]) for i in range(len(SL) + 1)]
 
         for a in range(4):
             cast(0, a, S)
@@ -302,15 +322,14 @@ def tile_dbrxattention_pa_kernel(tc, x, w_qkv_bytes, w_qkv_scale, out_0, out_1, 
         cast(2, 0, S)
         quant_x()
         quant_w(0, 0)
-        for b in sbanks(1)[:2]:
-            st(1, *b)
+        st(*stream[0], 0)
+        st(*stream[0], 1)
         for b in vbanks(1)[:3]:
             vtr(1, *b)
         for cg in range(5):
             nx = cg + 1
             fu = cg + 2
             vb_ = vbanks(nx)
-            sb_ = sbanks(nx)
             if cg > 0:
                 quant_w(cg, 0)
             quant_w(cg, 1)
@@ -318,42 +337,55 @@ def tile_dbrxattention_pa_kernel(tc, x, w_qkv_bytes, w_qkv_scale, out_0, out_1, 
                 release(cg - 1)
                 rope_sum(G, cg - 1, 0, 4)
                 clamp_store(G, cg - 1, 0, 4)
-                if cg + 3 < 6:
-                    cast(cg + 3, 3, G)
-            else:
-                cast(2, 2, G, True)
-                cast(2, 3, G)
-                cast(3, 3, G)
-            casts = [(cg + 3, a) for a in range(3)] if cg + 3 < 6 else []
-            if cg == 0:
-                casts = [(2, 1)] + casts
-            for i in range(8):
+            for c in CAST[cg]["G"]:
+                cast(c[0], c[1], G, cg == 0 and c == CAST[cg]["G"][0])
+            mine = list(range(bounds[cg], bounds[cg + 1]))
+            steps = []
+            cs = [[c[0], c[1], S] for c in CAST[cg]["S"]]
+            for n, i in enumerate(mine):
+                p = stream[i]
+                if n > 0:
+                    steps.append((st, (p[0], p[1], 0)))
+                steps.append((acts, (p[0], p[1], 0)))
+                if n > 0:
+                    steps.append((st, (p[0], p[1], 1)))
+                steps.append((acts, (p[0], p[1], 1)))
+                steps.append((weave_scalar, p))
+                if n == 0:
+                    for c in cs[:2]:
+                        steps.append((cast, c))
+            for c in cs[2:]:
+                steps.append((cast, c))
+            k = len(steps)
+            cuts = [k * i // 4 for i in range(5)]
+            for i in range(4):
                 if i < len(vb_):
                     vop(nx, *vb_[i])
                 if i + 3 < len(vb_):
                     vtr(nx, *vb_[i + 3])
-                if i < len(sb_):
-                    sop(nx, *sb_[i])
                 if i < 3:
                     multiply(cg, i)
-                if i + 2 < len(sb_):
-                    st(nx, *sb_[i + 2])
-                if i == 1:
-                    for c in casts:
-                        cast(*c, S)
+                for f, a in steps[cuts[i]:cuts[i + 1]]:
+                    f(*a)
+            for i in range(4, len(vb_)):
+                vop(nx, *vb_[i])
+                if i + 3 < len(vb_):
+                    vtr(nx, *vb_[i + 3])
             rope_product(cg, 0)
             multiply(cg, 3)
             if fu < 6:
                 for b in vbanks(fu)[:3]:
                     vtr(fu, *b)
-                for b in sbanks(fu)[:2]:
-                    st(fu, *b)
+            if cg + 1 < 5:
+                p = stream[bounds[cg + 1]]
+                st(*p, 0)
+                st(*p, 1)
             for t in range(1, NT):
                 rope_product(cg, t)
         new_res(4)
         rope_sum(V, 4, 0, 3)
         quant_w(5, 0)
-        tags = ["trv", "trv", "trv", "trs"]
+        tags = ["trv", "trv", "trv", "acc"]
         for t in range(NT):
             multiply(5, t, (0, 1), tags[t])
         quant_w(5, 1)

@@ -134,6 +134,18 @@ def tile_dbrxattention_pa_kernel(tc, x, w_qkv_bytes, w_qkv_scale, out_0, out_1, 
                 engine.tensor_copy(out=t[:], in_=src)
             wbf[(cg, a)] = t
 
+        zeros = const.tile([P, 512], BF16, name="zeros", tag="zeros")
+        nc.gpsimd.memset(zeros[:], 0.0)
+
+        def warm_plain(bank, n=1):
+            for i in range(n):
+                nc.tensor.matmul(bank[:], lhsT=zeros[:, 0:P], rhs=zeros[:], start=True, stop=True)
+
+        def warm_mx(bank, n=1):
+            for i in range(n):
+                nc.tensor.matmul_mx(out=bank[:], lhsT=xc[:, 0, 0:P].bitcast(FP8X4), lhsT_scale=xsc[:, 0, 0:P],
+                                    rhs=xc[:, 1, :].bitcast(FP8X4), rhs_scale=xsc[:, 1, :], start=True, stop=True)
+
         def half_tile(cg, h):
             if (cg, h) not in grp:
                 grp[(cg, h)] = work.tile([P, 2, D], BF16, name="gr", tag="gr%d" % h, bufs=2, align_bytes=64)
@@ -142,9 +154,13 @@ def tile_dbrxattention_pa_kernel(tc, x, w_qkv_bytes, w_qkv_scale, out_0, out_1, 
         vb = {}
         sb = {}
 
-        def vtr(cg, g, h, tag="trv"):
+        def vtr(cg, g, h, tag="trv", w=0):
             bank = psum.tile([P, 512], F32, name=tag, tag=tag, bufs=TAGS[tag])
             vb[(cg, g, h)] = bank
+            if w > 0:
+                warm_mx(bank, w)
+            if w < 0:
+                warm_plain(bank, -w)
             for u in range(2):
                 for a in range(2):
                     nc.tensor.transpose(bank[:, (2 * u + a) * P:(2 * u + a + 1) * P],
@@ -159,9 +175,13 @@ def tile_dbrxattention_pa_kernel(tc, x, w_qkv_bytes, w_qkv_scale, out_0, out_1, 
                 in1=s4[:, 4 * g:4 * g + 4].rearrange("p (u e) -> p u e", e=2).unsqueeze(1).to_broadcast([P, 256, 2, 2]),
                 op=ALU.mult)
 
-        def st(cg, g, u, tag="trs"):
+        def st(cg, g, u, tag="trs", w=0):
             bank = psum.tile([P, 512], F32, name=tag, tag=tag, bufs=TAGS[tag])
             sb[(cg, g, u)] = bank
+            if w > 0:
+                warm_mx(bank, w)
+            if w < 0:
+                warm_plain(bank, -w)
             for a in range(4):
                 nc.tensor.transpose(bank[:, a * P:(a + 1) * P],
                                     wbf[(cg, a)][:].bitcast(F32)[:, 256 * g + u:256 * (g + 1):2], ident[:])
@@ -172,18 +192,19 @@ def tile_dbrxattention_pa_kernel(tc, x, w_qkv_bytes, w_qkv_scale, out_0, out_1, 
 
         def acts(cg, g, u):
             if u == 0:
-                planes[(cg, g)] = work.tile([P, 4, 512], BF16, name="planes", tag="planes", bufs=3)
+                planes[(cg, g)] = work.tile([P, 2, 512, 2], BF16, name="planes", tag="planes", bufs=3)
             pl = planes[(cg, g)]
             bank = sb[(cg, g, u)]
             for e in range(2):
                 j = 2 * u + e
-                nc.scalar.activation(out=pl[:, j, :], in_=bank[:].bitcast(BF16)[:, e:1024:2],
+                nc.scalar.activation(out=pl[:, u, :, e], in_=bank[:].bitcast(BF16)[:, e:1024:2],
                                      func=ACT.Copy, scale=s4[:, 4 * g + j:4 * g + j + 1])
 
         def weave_scalar(cg, g):
             gr = half_tile(cg, g // 2)
-            nc.scalar.copy(out=gr[:, g % 2, :].rearrange("p (r j) -> p r j", j=4),
-                           in_=planes[(cg, g)][:].rearrange("p j r -> p r j"))
+            words = planes[(cg, g)][:].rearrange("p u r e -> p (u r e)").bitcast(F32)
+            nc.scalar.copy(out=gr[:, g % 2, :].bitcast(F32).rearrange("p (r u) -> p r u", u=2),
+                           in_=words.rearrange("p (u r) -> p r u", u=2))
 
         def weave_tensor(cg, g, c):
             bank = psum.tile([P, 1024], BF16, name="trs", tag="trs", bufs=TAGS["trs"])
@@ -197,11 +218,13 @@ def tile_dbrxattention_pa_kernel(tc, x, w_qkv_bytes, w_qkv_scale, out_0, out_1, 
             gr = half_tile(cg, g // 2)
             nc.scalar.copy(out=gr[:, g % 2, c * 1024:(c + 1) * 1024], in_=ib[(cg, g, c)][:])
 
-        def xbank(half, g):
+        def xbank(half, g, w=0):
             if not xgrp:
                 xgrp.append(work.tile([P, 2, 2, D], BF16, name="xg", tag="big", bufs=2, align_bytes=64))
             tag = "trs"
             bank = psum.tile([P, 512], F32, name=tag, tag=tag, bufs=TAGS[tag])
+            if w < 0:
+                warm_plain(bank, -w)
             for a in range(2):
                 for u in range(2):
                     nc.tensor.transpose(bank[:, (2 * a + u) * P:(2 * a + u + 1) * P],
@@ -227,7 +250,7 @@ def tile_dbrxattention_pa_kernel(tc, x, w_qkv_bytes, w_qkv_scale, out_0, out_1, 
             wcod[(cg, h)] = (c, s)
 
         def multiply(cg, t, passes=(0, 1, 2, 3), tag="acc"):
-            if passes[0] == 0:
+            if passes[0] == 0 and tag is not None:
                 acc[(cg, t)] = psum.tile([P, 512], F32, name=tag, tag=tag, bufs=TAGS[tag])
             for g in passes:
                 c, s = wcod[(cg, g // 2)]
@@ -241,14 +264,14 @@ def tile_dbrxattention_pa_kernel(tc, x, w_qkv_bytes, w_qkv_scale, out_0, out_1, 
                     stop=(g == NG - 1),
                 )
 
-        def store(cg, t, src):
+        def store(cg, t, src, queue=nc.sync):
             if cg < 4:
                 dst = out_0[0, 4 * cg:4 * cg + 4, t * P:(t + 1) * P, :]
             elif cg == 4:
                 dst = out_1[0, :, t * P:(t + 1) * P, :]
             else:
                 dst = out_2[0, :, t * P:(t + 1) * P, :]
-            nc.sync.dma_start(out=dst.rearrange("n p h -> p n h"), in_=src.rearrange("p (n h) -> p n h", n=4))
+            queue.dma_start(out=dst.rearrange("n p h -> p n h"), in_=src.rearrange("p (n h) -> p n h", n=4))
 
         prod = {}
         res = {}
@@ -286,13 +309,12 @@ def tile_dbrxattention_pa_kernel(tc, x, w_qkv_bytes, w_qkv_scale, out_0, out_1, 
             plain = work.tile([P, 512], F32, name="plain", tag="plain", bufs=4)
             nc.vector.tensor_scalar(out=plain[:], in0=acc[(cg, t)][:], scalar1=CLAMP, scalar2=-CLAMP,
                                     op0=ALU.min, op1=ALU.max)
-            store(cg, t, plain[:])
+            store(cg, t, plain[:], nc.scalar)
 
         V, S, G = nc.vector, nc.scalar, nc.gpsimd
         NV = [4,2,3,2,2,1]
         SL = [2,2,2,2,2]
-        CAST = [{"G":[[2,2],[2,3],[3,3]],"S":[[2,1],[3,0],[3,1],[3,2]]},{"G":[[4,3]],"S":[[4,0],[4,1],[4,2]]},{"G":[[5,3]],"S":[[5,0],[5,1],[5,2]]},{"G":[],"S":[]},{"G":[],"S":[]}]
-        PI = lambda cg, g: False
+        CAST = [{"G":[[2,2],[2,3],[3,3]],"S":[[2,1],[3,0],[3,1],[3,2]]},{"G":[],"S":[[4,0],[4,1],[4,2],[4,3]]},{"G":[],"S":[[5,0],[5,1],[5,2],[5,3]]},{"G":[],"S":[]},{"G":[],"S":[]}]
 
         def vbanks(cg):
             return [(g, h) for g in range(NV[cg]) for h in range(2)]
@@ -303,18 +325,18 @@ def tile_dbrxattention_pa_kernel(tc, x, w_qkv_bytes, w_qkv_scale, out_0, out_1, 
         for a in range(4):
             cast(0, a, S)
         for g in range(NG):
-            vtr(0, g, 0, "trv" if g % 2 == 0 else "acc")
+            vtr(0, g, 0, "trv" if g % 2 == 0 else "acc", 0)
         for g in range(NG):
             vop(0, g, 0)
         for g in range(NG):
-            xbank(0, g)
+            xbank(0, g, 0)
         for g in range(NG):
-            vtr(0, g, 1, "trv" if g % 2 == 0 else "acc")
+            vtr(0, g, 1, "trv" if g % 2 == 0 else "acc", 0)
         for g in range(NG):
             vop(0, g, 1)
         tables_second_part()
         for g in range(NG):
-            xbank(1, g)
+            xbank(1, g, 0)
         cast(1, 2, G)
         cast(1, 0, S)
         cast(1, 1, S)
@@ -322,21 +344,22 @@ def tile_dbrxattention_pa_kernel(tc, x, w_qkv_bytes, w_qkv_scale, out_0, out_1, 
         cast(2, 0, S)
         quant_x()
         quant_w(0, 0)
-        st(*stream[0], 0)
-        st(*stream[0], 1)
+        st(*stream[0], 0, w=0)
+        st(*stream[0], 1, w=0)
         for b in vbanks(1)[:3]:
-            vtr(1, *b)
+            vtr(1, *b, w=0)
+        multiply(0, 0, (0, 1))
+        multiply(0, 1, (0, 1))
         for cg in range(5):
             nx = cg + 1
             fu = cg + 2
             vb_ = vbanks(nx)
-            if cg > 0:
-                quant_w(cg, 0)
             quant_w(cg, 1)
             if cg >= 1:
                 release(cg - 1)
-                rope_sum(G, cg - 1, 0, 4)
-                clamp_store(G, cg - 1, 0, 4)
+                for t in (0, 2):
+                    rope_sum(G, cg - 1, t, t + 2)
+                    clamp_store(G, cg - 1, t, t + 2)
             for c in CAST[cg]["G"]:
                 cast(c[0], c[1], G, cg == 0 and c == CAST[cg]["G"][0])
             mine = list(range(bounds[cg], bounds[cg + 1]))
@@ -352,47 +375,58 @@ def tile_dbrxattention_pa_kernel(tc, x, w_qkv_bytes, w_qkv_scale, out_0, out_1, 
                 steps.append((acts, (p[0], p[1], 1)))
                 steps.append((weave_scalar, p))
                 if n == 0:
-                    for c in cs[:2]:
+                    for c in cs[:3]:
                         steps.append((cast, c))
-            for c in cs[2:]:
+            for c in cs[3:]:
                 steps.append((cast, c))
             k = len(steps)
             cuts = [k * i // 4 for i in range(5)]
+            mms = [(0, (2, 3)), (1, (2, 3)), (2, (0, 1, 2, 3))]
             for i in range(4):
                 if i < len(vb_):
                     vop(nx, *vb_[i])
-                if i + 3 < len(vb_):
-                    vtr(nx, *vb_[i + 3])
                 if i < 3:
-                    multiply(cg, i)
+                    multiply(cg, *mms[i])
+                if i + 3 < len(vb_):
+                    vtr(nx, *vb_[i + 3], w=0)
                 for f, a in steps[cuts[i]:cuts[i + 1]]:
                     f(*a)
             for i in range(4, len(vb_)):
                 vop(nx, *vb_[i])
                 if i + 3 < len(vb_):
-                    vtr(nx, *vb_[i + 3])
+                    vtr(nx, *vb_[i + 3], w=0)
             rope_product(cg, 0)
-            multiply(cg, 3)
+            multiply(cg, 3, (0, 1))
             if fu < 6:
-                for b in vbanks(fu)[:3]:
-                    vtr(fu, *b)
+                for b in vbanks(fu)[:1]:
+                    vtr(fu, *b, w=0)
+            multiply(cg, 3, (2, 3))
+            if fu < 6:
+                for b in vbanks(fu)[1:3]:
+                    vtr(fu, *b, w=0)
             if cg + 1 < 5:
                 p = stream[bounds[cg + 1]]
-                st(*p, 0)
-                st(*p, 1)
-            for t in range(1, NT):
-                rope_product(cg, t)
+                st(*p, 0, w=0)
+                st(*p, 1, w=0)
+            rope_product(cg, 1)
+            rope_product(cg, 2)
+            quant_w(nx, 0)
+            if nx < 5:
+                multiply(nx, 0, (0, 1))
+                multiply(nx, 1, (0, 1))
+            rope_product(cg, 3)
         new_res(4)
-        rope_sum(V, 4, 0, 3)
-        quant_w(5, 0)
         tags = ["trv", "trv", "trv", "acc"]
         for t in range(NT):
-            multiply(5, t, (0, 1), tags[t])
+            acc[(5, t)] = psum.tile([P, 512], F32, name=tags[t], tag=tags[t], bufs=TAGS[tags[t]])
+            warm_mx(acc[(5, t)], 0)
+            multiply(5, t, (0, 1), None)
+        rope_sum(V, 4, 0, 2)
         quant_w(5, 1)
-        clamp_store(V, 4, 0, 3)
-        nc.vector.memset(res[4][:, 3, 0:1], 0.0)
-        rope_sum(G, 4, 3, 4)
-        clamp_store(G, 4, 3, 4)
+        clamp_store(V, 4, 0, 2)
+        nc.vector.memset(res[4][:, 2, 0:1], 0.0)
+        rope_sum(G, 4, 2, 4)
+        clamp_store(G, 4, 2, 4)
         for t in range(NT):
             multiply(5, t, (2, 3))
             finish_plain(5, t)

@@ -235,11 +235,10 @@ def tile_dbrxattention_pa_kernel(tc, x, w_qkv_bytes, w_qkv_scale, out_0, out_1, 
                 in_=bank[:].rearrange("p (a u r) -> p a r u", a=2, u=2),
             )
 
-        def quant_x():
-            for h in range(2):
-                nc.vector.quantize_mx(out=xc[:, 2 * h:2 * h + 2, :].rearrange("p h c -> p (h c)").bitcast(FP8X4),
-                                      scales=xsc[:, 2 * h:2 * h + 2, :].rearrange("p h c -> p (h c)"),
-                                      in_=xgrp[0][:, h, :, :].rearrange("p h c -> p (h c)"))
+        def quant_x(h):
+            nc.vector.quantize_mx(out=xc[:, 2 * h:2 * h + 2, :].rearrange("p h c -> p (h c)").bitcast(FP8X4),
+                                  scales=xsc[:, 2 * h:2 * h + 2, :].rearrange("p h c -> p (h c)"),
+                                  in_=xgrp[0][:, h, :, :].rearrange("p h c -> p (h c)"))
 
         def quant_w(cg, h):
             c = work.tile([P, 2, 512], U32, name="wc", tag="wc", bufs=4, align_bytes=64)
@@ -314,7 +313,7 @@ def tile_dbrxattention_pa_kernel(tc, x, w_qkv_bytes, w_qkv_scale, out_0, out_1, 
         V, S, G = nc.vector, nc.scalar, nc.gpsimd
         NV = [4,2,3,2,2,1]
         SL = [2,2,2,2,2]
-        CAST = [{"G":[[2,2],[2,3],[3,3]],"S":[[2,1],[3,0],[3,1],[3,2]]},{"G":[],"S":[[4,0],[4,1],[4,2],[4,3]]},{"G":[],"S":[[5,0],[5,1],[5,2],[5,3]]},{"G":[],"S":[]},{"G":[],"S":[]}]
+        CAST = [{"G":[[2,1],[2,2],[2,3],[3,3]],"S":[[3,0],[3,1],[3,2]]},{"G":[],"S":[[4,0],[4,1],[4,2],[4,3]]},{"G":[],"S":[[5,0],[5,1],[5,2],[5,3]]},{"G":[],"S":[]},{"G":[],"S":[]}]
 
         def vbanks(cg):
             return [(g, h) for g in range(NV[cg]) for h in range(2)]
@@ -325,31 +324,34 @@ def tile_dbrxattention_pa_kernel(tc, x, w_qkv_bytes, w_qkv_scale, out_0, out_1, 
         for a in range(4):
             cast(0, a, S)
         for g in range(NG):
-            vtr(0, g, 0, "trv" if g % 2 == 0 else "acc", 0)
+            vtr(0, g, 0, "trv" if g % 2 == 0 else "acc")
         for g in range(NG):
             vop(0, g, 0)
+        for g in range(2):
+            xbank(0, g)
+            xbank(1, g)
+        quant_x(0)
+        cast(1, 2, G, True)
+        cast(1, 3, G)
         for g in range(NG):
-            xbank(0, g, 0)
-        for g in range(NG):
-            vtr(0, g, 1, "trv" if g % 2 == 0 else "acc", 0)
+            vtr(0, g, 1, "trv" if g % 2 == 0 else "acc")
         for g in range(NG):
             vop(0, g, 1)
-        tables_second_part()
-        for g in range(NG):
-            xbank(1, g, 0)
-        cast(1, 2, G)
         cast(1, 0, S)
         cast(1, 1, S)
-        cast(1, 3, G)
-        cast(2, 0, S)
-        quant_x()
+        for g in range(2, NG):
+            xbank(0, g)
+            xbank(1, g)
+        tables_second_part()
         quant_w(0, 0)
-        st(*stream[0], 0, w=0)
-        st(*stream[0], 1, w=0)
+        quant_x(1)
         for b in vbanks(1)[:3]:
-            vtr(1, *b, w=0)
+            vtr(1, *b)
+        st(*stream[0], 0)
+        st(*stream[0], 1)
         multiply(0, 0, (0, 1))
         multiply(0, 1, (0, 1))
+        cast(2, 0, S)
         for cg in range(5):
             nx = cg + 1
             fu = cg + 2
@@ -375,9 +377,9 @@ def tile_dbrxattention_pa_kernel(tc, x, w_qkv_bytes, w_qkv_scale, out_0, out_1, 
                 steps.append((acts, (p[0], p[1], 1)))
                 steps.append((weave_scalar, p))
                 if n == 0:
-                    for c in cs[:3]:
+                    for c in cs[:1 if cg == 0 else 3]:
                         steps.append((cast, c))
-            for c in cs[3:]:
+            for c in cs[1 if cg == 0 else 3:]:
                 steps.append((cast, c))
             k = len(steps)
             cuts = [k * i // 4 for i in range(5)]
@@ -425,8 +427,9 @@ def tile_dbrxattention_pa_kernel(tc, x, w_qkv_bytes, w_qkv_scale, out_0, out_1, 
         quant_w(5, 1)
         clamp_store(V, 4, 0, 2)
         nc.vector.memset(res[4][:, 2, 0:1], 0.0)
-        rope_sum(G, 4, 2, 4)
-        clamp_store(G, 4, 2, 4)
+        for t in range(2, NT):
+            rope_sum(G, 4, t, t + 1)
+            clamp_store(G, 4, t, t + 1)
         for t in range(NT):
             multiply(5, t, (2, 3))
             finish_plain(5, t)

from contextlib import ExitStack
import math

import concourse.mybir as mybir
from concourse.masks import make_identity

T, D, O = 512, 2048, 3072
HD = 128
FLOPS = 2 * T * D * O

F32 = mybir.dt.float32
BF16 = mybir.dt.bfloat16
U32 = mybir.dt.uint32
U8 = mybir.dt.uint8
I32 = mybir.dt.int32
FP8 = mybir.dt.float8_e4m3fn
FP8X4 = mybir.dt.float8_e4m3fn_x4
ALU = mybir.AluOpType
ACT = mybir.ActivationFunctionType

P = 128
NG = 4
NT = 4
CLAMP = 8.0
ROPE_BASE = 500000.0
PI_HI = 3.140625
PI_LO = math.pi - PI_HI


TAGS = {"trv": 3, "trs": 2, "acc": 3}
WBF = 11


def tile_dbrxattention_pa_kernel(tc, x, w_qkv_bytes, w_qkv_scale, out_0, out_1, out_2):
    nc = tc.nc
    with ExitStack() as ctx:
        const = ctx.enter_context(tc.tile_pool(name="const", bufs=1))
        work = ctx.enter_context(tc.tile_pool(name="work", bufs=2))
        psum = ctx.enter_context(tc.psum_pool(name="psum", bufs=4))
        ctx.enter_context(tc.manual_schedule())

        wb = {}
        s4 = const.tile([P, 4 * NG], F32, name="s4", tag="s4")
        xs = work.tile([P, NT, D], BF16, name="xs", tag="big", bufs=2, align_bytes=64)
        nc.sync.dma_start(out=s4[:].rearrange("p (g t) -> p g t", t=4),
                          in_=w_qkv_scale.rearrange("o (g p t) -> p (o g) t", p=P, t=4))

        def load_w(cg, a0, a1):
            if cg not in wb:
                wb[cg] = work.tile([P, 4, D], U8, name="wbytes", tag="wbytes", bufs=4)
            nc.sync.dma_start(
                out=wb[cg][:, a0:a1, :],
                in_=w_qkv_bytes[cg * 512 + a0 * P:cg * 512 + a1 * P, :].rearrange("(a p) k -> p a k", p=P),
            )

        def load_x(t):
            nc.sync.dma_start(out=xs[:, t, :], in_=x[0, t * P:(t + 1) * P, :])

        tpos = const.tile([P, NT], F32, name="tpos", tag="tpos")
        nc.gpsimd.iota(tpos[:], pattern=[[P, NT]], base=0, channel_multiplier=1,
                       allow_small_or_imprecise_dtypes=True)
        ident = const.tile([P, P], F32, name="ident", tag="ident")
        make_identity(nc, ident[:])

        load_w(0, 0, 1)
        load_w(0, 1, 2)
        load_w(0, 2, 3)
        load_w(0, 3, 4)
        load_x(0)
        load_x(1)
        load_x(2)
        load_x(3)
        load_w(1, 0, 4)
        load_w(2, 0, 4)
        load_w(3, 0, 4)
        load_w(4, 0, 4)
        load_w(5, 0, 4)

        warm = const.tile([P, 2], F32, name="warm", tag="warm")
        nc.vector.memset(warm[:, 0:1], 0.0)
        nc.scalar.activation(out=warm[:, 1:2], in_=warm[:, 0:1], func=ACT.Sin)

        q = ROPE_BASE ** (-2.0 / HD)
        angs = const.tile([P, 2, NT, 64], F32, name="angs", tag="angs")
        nc.vector.tensor_copy(out=angs[:, 0, :, 0:1], in_=tpos[:].unsqueeze(2))
        for j in range(6):
            w = 2 ** j
            nc.vector.tensor_scalar(out=angs[:, 0, :, w:2 * w], in0=angs[:, 0, :, 0:w], scalar1=q ** w,
                                    scalar2=None, op0=ALU.mult)
        nc.vector.tensor_scalar(out=angs[:, 1, :, :], in0=angs[:, 0, :, :], scalar1=0.5 * math.pi,
                                scalar2=None, op0=ALU.add)
        angf = angs[:].rearrange("p s t i -> p (s t i)")
        m_i = const.tile([P, 512], I32, name="m_i", tag="m_i")
        nc.vector.tensor_scalar(out=m_i[:], in0=angf, scalar1=1.0 / math.pi, scalar2=0.25,
                                op0=ALU.mult, op1=ALU.add)
        red = const.tile([P, 512], F32, name="red", tag="red")
        nc.vector.scalar_tensor_tensor(out=red[:], in0=m_i[:], scalar=-PI_HI, in1=angf,
                                       op0=ALU.mult, op1=ALU.add)
        red2 = const.tile([P, 512], F32, name="red2", tag="red2")
        nc.vector.scalar_tensor_tensor(out=red2[:], in0=m_i[:], scalar=-PI_LO, in1=red[:],
                                       op0=ALU.mult, op1=ALU.add)
        b_i = const.tile([P, 512], I32, name="b_i", tag="b_i")
        nc.vector.tensor_scalar(out=b_i[:], in0=m_i[:], scalar1=1, scalar2=None, op0=ALU.bitwise_and)
        sg = const.tile([P, 512], F32, name="sg", tag="sg")
        nc.vector.tensor_scalar(out=sg[:], in0=b_i[:], scalar1=-2.0, scalar2=1.0, op0=ALU.mult, op1=ALU.add)
        arg = const.tile([P, 2, NT, 64], F32, name="arg", tag="arg")
        nc.vector.tensor_tensor(out=arg[:].rearrange("p s t i -> p (s t i)"), in0=red2[:], in1=sg[:], op=ALU.mult)
        tab = const.tile([P, NT, 2, 64, 2], F32, name="tab", tag="tab")

        def tables_second_part():
            nc.scalar.activation(
                out=tab[:, :, 0, :, :].rearrange("p t i e -> p t (i e)").rearrange("p t (i e) -> p t i e", e=2),
                in_=arg[:, 1, :, :].unsqueeze(3).to_broadcast([P, NT, 64, 2]), func=ACT.Sin)
            nc.scalar.activation(out=tab[:, :, 1, :, 0], in_=arg[:, 0, :, :], func=ACT.Sin)
            nc.scalar.activation(out=tab[:, :, 1, :, 1], in_=arg[:, 0, :, :], func=ACT.Sin, scale=-1.0)

        xc = const.tile([P, NG, T], U32, name="xc", tag="xc", align_bytes=64)
        xsc = const.tile([P, NG, T], U8, name="xsc", tag="xsc", align_bytes=64)
        wbf = {}
        grp = {}
        wcod = {}
        acc = {}
        planes = {}
        xgrp = []

        def cast(cg, a, engine, held=False):
            t = work.tile([P, D], BF16, name="wbf", tag="wbf", bufs=WBF)
            if held:
                nc.vector.memset(t[:, 0:2], 0.0)
            src = wb[cg][:, a, :].bitcast(FP8)
            if engine is nc.scalar:
                nc.scalar.copy(out=t[:], in_=src)
            else:
                engine.tensor_copy(out=t[:], in_=src)
            wbf[(cg, a)] = t

        zeros = const.tile([P, 512], BF16, name="zeros", tag="zeros")
        nc.gpsimd.memset(zeros[:], 0.0)

        def warm_plain(bank, n=1):
            for i in range(n):
                nc.tensor.matmul(bank[:], lhsT=zeros[:, 0:P], rhs=zeros[:], start=True, stop=True)

        def warm_mx(bank, n=1):
            for i in range(n):
                nc.tensor.matmul_mx(out=bank[:], lhsT=xc[:, 0, 0:P].bitcast(FP8X4), lhsT_scale=xsc[:, 0, 0:P],
                                    rhs=xc[:, 1, :].bitcast(FP8X4), rhs_scale=xsc[:, 1, :], start=True, stop=True)

        def half_tile(cg, h):
            if (cg, h) not in grp:
                grp[(cg, h)] = work.tile([P, 2, D], BF16, name="gr", tag="gr%d" % h, bufs=2, align_bytes=64)
            return grp[(cg, h)]

        vb = {}
        sb = {}

        def vtr(cg, g, h, tag="trv", w=0):
            bank = psum.tile([P, 512], F32, name=tag, tag=tag, bufs=TAGS[tag])
            vb[(cg, g, h)] = bank
            if w > 0:
                warm_mx(bank, w)
            if w < 0:
                warm_plain(bank, -w)
            for u in range(2):
                for a in range(2):
                    nc.tensor.transpose(bank[:, (2 * u + a) * P:(2 * u + a + 1) * P],
                                        wbf[(cg, 2 * h + a)][:].bitcast(F32)[:, 256 * g + u:256 * (g + 1):2], ident[:])

        def vop(cg, g, h):
            gr = half_tile(cg, g // 2)
            bank = vb[(cg, g, h)]
            nc.vector.tensor_tensor(
                out=gr[:, g % 2, h * 1024:(h + 1) * 1024].rearrange("p (r u e) -> p r u e", u=2, e=2),
                in0=bank[:].bitcast(BF16).rearrange("p (u r e) -> p r u e", u=2, e=2),
                in1=s4[:, 4 * g:4 * g + 4].rearrange("p (u e) -> p u e", e=2).unsqueeze(1).to_broadcast([P, 256, 2, 2]),
                op=ALU.mult)

        def st(cg, g, u, tag="trs", w=0):
            bank = psum.tile([P, 512], F32, name=tag, tag=tag, bufs=TAGS[tag])
            sb[(cg, g, u)] = bank
            if w > 0:
                warm_mx(bank, w)
            if w < 0:
                warm_plain(bank, -w)
            for a in range(4):
                nc.tensor.transpose(bank[:, a * P:(a + 1) * P],
                                    wbf[(cg, a)][:].bitcast(F32)[:, 256 * g + u:256 * (g + 1):2], ident[:])

        identb = const.tile([P, P], BF16, name="identb", tag="identb")
        make_identity(nc, identb[:])
        ib = {}

        def acts(cg, g, u):
            if u == 0:
                planes[(cg, g)] = work.tile([P, 2, 512, 2], BF16, name="planes", tag="planes", bufs=3)
            pl = planes[(cg, g)]
            bank = sb[(cg, g, u)]
            for e in range(2):
                j = 2 * u + e
                nc.scalar.activation(out=pl[:, u, :, e], in_=bank[:].bitcast(BF16)[:, e:1024:2],
                                     func=ACT.Copy, scale=s4[:, 4 * g + j:4 * g + j + 1])

        def weave_scalar(cg, g):
            gr = half_tile(cg, g // 2)
            words = planes[(cg, g)][:].rearrange("p u r e -> p (u r e)").bitcast(F32)
            nc.scalar.copy(out=gr[:, g % 2, :].bitcast(F32).rearrange("p (r u) -> p r u", u=2),
                           in_=words.rearrange("p (u r) -> p r u", u=2))

        def weave_tensor(cg, g, c):
            bank = psum.tile([P, 1024], BF16, name="trs", tag="trs", bufs=TAGS["trs"])
            ib[(cg, g, c)] = bank
            for q in range(2):
                rows = slice((2 * c + q) * P, (2 * c + q + 1) * P)
                nc.tensor.matmul(bank[:, q * 512:(q + 1) * 512].rearrange("p (r j) -> p r j", j=4), lhsT=identb[:],
                                 rhs=planes[(cg, g)][:, :, rows].rearrange("p j r -> p r j"), start=True, stop=True)

        def weave_out(cg, g, c):
            gr = half_tile(cg, g // 2)
            nc.scalar.copy(out=gr[:, g % 2, c * 1024:(c + 1) * 1024], in_=ib[(cg, g, c)][:])

        def xbank(half, g, w=0):
            if not xgrp:
                xgrp.append(work.tile([P, 2, 2, D], BF16, name="xg", tag="big", bufs=2, align_bytes=64))
            tag = "trs"
            bank = psum.tile([P, 512], F32, name=tag, tag=tag, bufs=TAGS[tag])
            if w < 0:
                warm_plain(bank, -w)
            for a in range(2):
                for u in range(2):
                    nc.tensor.transpose(bank[:, (2 * a + u) * P:(2 * a + u + 1) * P],
                                        xs[:, 2 * half + a, :].bitcast(F32)[:, 256 * g + u:256 * (g + 1):2], ident[:])
            nc.scalar.copy(
                out=xgrp[0][:, g // 2, g % 2, :].bitcast(F32)[:, half * 512:(half + 1) * 512].rearrange(
                    "p (a r u) -> p a r u", a=2, u=2),
                in_=bank[:].rearrange("p (a u r) -> p a r u", a=2, u=2),
            )

        def quant_x(h):
            nc.vector.quantize_mx(out=xc[:, 2 * h:2 * h + 2, :].rearrange("p h c -> p (h c)").bitcast(FP8X4),
                                  scales=xsc[:, 2 * h:2 * h + 2, :].rearrange("p h c -> p (h c)"),
                                  in_=xgrp[0][:, h, :, :].rearrange("p h c -> p (h c)"))

        def quant_w(cg, h):
            c = work.tile([P, 2, 512], U32, name="wc", tag="wc", bufs=4, align_bytes=64)
            s = work.tile([P, 2, 512], U8, name="ws", tag="ws", bufs=4, align_bytes=64)
            nc.vector.quantize_mx(out=c[:].rearrange("p h c -> p (h c)").bitcast(FP8X4),
                                  scales=s[:].rearrange("p h c -> p (h c)"),
                                  in_=grp[(cg, h)][:].rearrange("p h c -> p (h c)"))
            wcod[(cg, h)] = (c, s)

        def multiply(cg, t, passes=(0, 1, 2, 3), tag="acc"):
            if passes[0] == 0 and tag is not None:
                acc[(cg, t)] = psum.tile([P, 512], F32, name=tag, tag=tag, bufs=TAGS[tag])
            for g in passes:
                c, s = wcod[(cg, g // 2)]
                nc.tensor.matmul_mx(
                    out=acc[(cg, t)][:],
                    lhsT=xc[:, g, t * P:(t + 1) * P].bitcast(FP8X4),
                    lhsT_scale=xsc[:, g, t * P:(t + 1) * P],
                    rhs=c[:, g % 2, :].bitcast(FP8X4),
                    rhs_scale=s[:, g % 2, :],
                    start=(g == 0),
                    stop=(g == NG - 1),
                )

        def store(cg, t, src, queue=nc.sync):
            if cg < 4:
                dst = out_0[0, 4 * cg:4 * cg + 4, t * P:(t + 1) * P, :]
            elif cg == 4:
                dst = out_1[0, :, t * P:(t + 1) * P, :]
            else:
                dst = out_2[0, :, t * P:(t + 1) * P, :]
            queue.dma_start(out=dst.rearrange("n p h -> p n h"), in_=src.rearrange("p (n h) -> p n h", n=4))

        prod = {}
        res = {}

        def rope_product(cg, t):
            if t == 0:
                prod[cg] = work.tile([P, NT, 2, 512], F32, name="prod", tag="big", bufs=2, align_bytes=64)
            nc.vector.tensor_tensor(
                out=prod[cg][:, t, :, :].rearrange("p s (n h) -> p s n h", n=4),
                in0=acc[(cg, t)][:].rearrange("p (n h) -> p n h", n=4).unsqueeze(1).to_broadcast([P, 2, 4, HD]),
                in1=tab[:, t, :, :, :].rearrange("p s i e -> p s (i e)").unsqueeze(2).to_broadcast([P, 2, 4, HD]),
                op=ALU.mult)

        def rope_sum(engine, cg, t0, t1):
            engine.tensor_tensor(
                out=res[cg][:, t0:t1, :].rearrange("p t (m e) -> p t m e", e=2),
                in0=prod[cg][:, t0:t1, 0, :].rearrange("p t (m e) -> p t m e", e=2),
                in1=prod[cg][:, t0:t1, 1, :].rearrange("p t (m e) -> p t m e", e=2)[:, :, :, ::-1],
                op=ALU.add)

        def clamp_store(engine, cg, t0, t1):
            engine.tensor_scalar(out=res[cg][:, t0:t1, :], in0=res[cg][:, t0:t1, :], scalar1=CLAMP, scalar2=-CLAMP,
                                 op0=ALU.min, op1=ALU.max)
            for t in range(t0, t1):
                store(cg, t, res[cg][:, t, :])

        def new_res(cg):
            res[cg] = work.tile([P, NT, 512], F32, name="res", tag="res", bufs=3)

        def release(cg):
            new_res(cg)
            nc.vector.memset(res[cg][:, 0, 0:1], 0.0)

        def finish_plain(cg, t):
            plain = work.tile([P, 512], F32, name="plain", tag="plain", bufs=4)
            nc.vector.tensor_scalar(out=plain[:], in0=acc[(cg, t)][:], scalar1=CLAMP, scalar2=-CLAMP,
                                    op0=ALU.min, op1=ALU.max)
            store(cg, t, plain[:], nc.scalar)

        V, S, G = nc.vector, nc.scalar, nc.gpsimd
        NV = [4,2,3,2,2,1]
        SL = [2,2,2,2,2]
        CAST = [{"G":[[2,1],[2,2],[2,3],[3,3]],"S":[[3,0],[3,1],[3,2]]},{"G":[],"S":[[4,0],[4,1],[4,2],[4,3]]},{"G":[],"S":[[5,0],[5,1],[5,2],[5,3]]},{"G":[],"S":[]},{"G":[],"S":[]}]

        def vbanks(cg):
            return [(g, h) for g in range(NV[cg]) for h in range(2)]

        stream = [(cg, g) for cg in range(1, 6) for g in range(NV[cg], 4)]
        bounds = [sum(SL[:i]) for i in range(len(SL) + 1)]

        for a in range(4):
            cast(0, a, S)
        for g in range(NG):
            vtr(0, g, 0, "trv" if g % 2 == 0 else "acc")
        for g in range(NG):
            vop(0, g, 0)
        for g in range(2):
            xbank(0, g)
            xbank(1, g)
        quant_x(0)
        cast(1, 2, G, True)
        cast(1, 3, G)
        for g in range(NG):
            vtr(0, g, 1, "trv" if g % 2 == 0 else "acc")
        for g in range(NG):
            vop(0, g, 1)
        cast(1, 0, S)
        cast(1, 1, S)
        for g in range(2, NG):
            xbank(0, g)
            xbank(1, g)
        tables_second_part()
        quant_w(0, 0)
        quant_x(1)
        for b in vbanks(1)[:3]:
            vtr(1, *b)
        st(*stream[0], 0)
        st(*stream[0], 1)
        multiply(0, 0, (0, 1))
        multiply(0, 1, (0, 1))
        cast(2, 0, S)
        for cg in range(5):
            nx = cg + 1
            fu = cg + 2
            vb_ = vbanks(nx)
            quant_w(cg, 1)
            if cg >= 1:
                release(cg - 1)
                for t in (0, 2):
                    rope_sum(G, cg - 1, t, t + 2)
                    clamp_store(G, cg - 1, t, t + 2)
            for c in CAST[cg]["G"]:
                cast(c[0], c[1], G, cg == 0 and c == CAST[cg]["G"][0])
            mine = list(range(bounds[cg], bounds[cg + 1]))
            steps = []
            cs = [[c[0], c[1], S] for c in CAST[cg]["S"]]
            for n, i in enumerate(mine):
                p = stream[i]
                if n > 0:
                    steps.append((st, (p[0], p[1], 0)))
                steps.append((acts, (p[0], p[1], 0)))
                if n > 0:
                    steps.append((st, (p[0], p[1], 1)))
                steps.append((acts, (p[0], p[1], 1)))
                steps.append((weave_scalar, p))
                if n == 0:
                    for c in cs[:1 if cg == 0 else 3]:
                        steps.append((cast, c))
            for c in cs[1 if cg == 0 else 3:]:
                steps.append((cast, c))
            k = len(steps)
            cuts = [k * i // 4 for i in range(5)]
            mms = [(0, (2, 3)), (1, (2, 3)), (2, (0, 1, 2, 3))]
            for i in range(4):
                if i < len(vb_):
                    vop(nx, *vb_[i])
                if i < 3:
                    multiply(cg, *mms[i])
                if i + 3 < len(vb_):
                    vtr(nx, *vb_[i + 3], w=0)
                for f, a in steps[cuts[i]:cuts[i + 1]]:
                    f(*a)
            for i in range(4, len(vb_)):
                vop(nx, *vb_[i])
                if i + 3 < len(vb_):
                    vtr(nx, *vb_[i + 3], w=0)
            rope_product(cg, 0)
            multiply(cg, 3, (0, 1))
            if fu < 6:
                for b in vbanks(fu)[:1]:
                    vtr(fu, *b, w=0)
            multiply(cg, 3, (2, 3))
            if fu < 6:
                for b in vbanks(fu)[1:3]:
                    vtr(fu, *b, w=0)
            if cg + 1 < 5:
                p = stream[bounds[cg + 1]]
                st(*p, 0, w=0)
                st(*p, 1, w=0)
            rope_product(cg, 1)
            rope_product(cg, 2)
            quant_w(nx, 0)
            if nx < 5:
                multiply(nx, 0, (0, 1))
                multiply(nx, 1, (0, 1))
            rope_product(cg, 3)
        new_res(4)
        tags = ["trv", "trv", "trv", "acc"]
        for t in range(NT):
            acc[(5, t)] = psum.tile([P, 512], F32, name=tags[t], tag=tags[t], bufs=TAGS[tags[t]])
            warm_mx(acc[(5, t)], 0)
            multiply(5, t, (0, 1), None)
        rope_sum(V, 4, 0, 2)
        quant_w(5, 1)
        clamp_store(V, 4, 0, 2)
        nc.vector.memset(res[4][:, 2, 0:1], 0.0)
        for t in range(2, NT):
            rope_sum(G, 4, t, t + 1)
            clamp_store(G, 4, t, t + 1)
        for t in range(NT):
            multiply(5, t, (2, 3))
            finish_plain(5, t)
